import numpy as np
import ml_dtypes


def mxq(x, axis, fmt="e4m3"):
    dtype, down = {"e4m3": (ml_dtypes.float8_e4m3fn, 7), "e5m2": (ml_dtypes.float8_e5m2, 14)}[fmt]
    v = np.moveaxis(np.asarray(x, np.float32).astype(ml_dtypes.bfloat16).astype(np.float64), axis, -1)
    blocks = v.reshape(v.shape[:-1] + (-1, 32))
    amax = np.abs(blocks).max(-1, keepdims=True)
    byte = np.maximum(np.where(amax > 0, np.frexp(amax)[1] - 1 + 127, 0) - down, 1)
    scale = np.exp2(byte - 127.0)
    codes = (blocks / scale).astype(np.float32).astype(dtype).astype(np.float64)
    return np.moveaxis((codes * scale).reshape(v.shape), -1, axis)


WIDE = False


def mx_kscale(k):
    if not WIDE:
        return np.ones(k)
    levels = np.array([10, -10, 5, -5, 0])
    a = np.random.permutation(np.resize(levels, k // 512 * 4)).reshape(k // 512, 4)
    idx = np.arange(k)
    return np.exp2(a[idx // 512, idx % 128 // 32])


BF16 = ml_dtypes.bfloat16


def bf(x):
    return np.asarray(x, np.float32).astype(BF16)


def f64(x):
    return np.asarray(x).astype(np.float64)


N, WI, H, DH, WO = 4096, 512, 2, 512, 256
F = WO // H
EPSILON = 1e-06
XS = 0.002


def setup_inputs():
    s = mx_kscale(WI)
    return {"x": bf(np.random.standard_normal((N, WI)) * XS * s),
            "norm_bias": bf(np.random.standard_normal((N, H, DH))),
            "w_lin": bf(np.random.standard_normal((WI, H * DH)) / np.sqrt(WI) / s[:, None]),
            "kernel": bf(np.random.standard_normal((H, DH, F)) / np.sqrt(DH))}


def reference(x, norm_bias, w_lin, kernel):
    xx = mxq(f64(x), 1, "e4m3") @ mxq(f64(w_lin), 0, "e4m3")
    xx = xx.reshape(N, H, DH)
    xx = xx / np.sqrt(np.mean(np.square(xx), axis=-1, keepdims=True) + EPSILON)
    xx = (xx + f64(norm_bias).reshape(xx.shape)) / np.sqrt(2.0)
    xh = xx.transpose(1, 0, 2)
    y = mxq(xh, 2, "e4m3") @ mxq(f64(kernel), 1, "e4m3")
    return y.transpose(1, 0, 2).reshape(N, H * F)

@@ -1,0 +1,282 @@
+import math
+from contextlib import ExitStack
+
+import concourse.mybir as mybir
+from concourse.masks import make_identity
+
+F32 = mybir.dt.float32
+BF16 = mybir.dt.bfloat16
+U32 = mybir.dt.uint32
+U8 = mybir.dt.uint8
+FP8X4 = mybir.dt.float8_e4m3fn_x4
+ACT = mybir.ActivationFunctionType
+ALU = mybir.AluOpType
+
+P = 128
+PACK = 4
+TOKENS = 4096
+K_IN = 512
+HEADS = 2
+D_HEAD = 512
+F_OUT = 128
+EPSILON = 1e-06
+
+HALVES = 2
+TILES = TOKENS // P
+TILES_PER_ROUND = 2
+ROUNDS = TILES // TILES_PER_ROUND
+UNITS = TILES_PER_ROUND * HEADS
+LOAD_AHEAD = 3
+LAST_STAGE = 5
+
+FLOPS = 2 * TOKENS * K_IN * HEADS * D_HEAD + 2 * TOKENS * HEADS * D_HEAD * F_OUT
+
+
+def tile_grouplinearblock_pa_t_kernel(tc, x, norm_bias, w_lin, kernel, out):
+    nc = tc.nc
+    with ExitStack() as ctx:
+        ctx.enter_context(tc.manual_schedule())
+        consts = ctx.enter_context(tc.tile_pool(name="consts", bufs=1))
+        loads = ctx.enter_context(tc.tile_pool(name="loads", bufs=LOAD_AHEAD + 3))
+        work = ctx.enter_context(tc.tile_pool(name="work", bufs=2))
+        ring3 = ctx.enter_context(tc.tile_pool(name="ring3", bufs=3))
+        ring4 = ctx.enter_context(tc.tile_pool(name="ring4", bufs=4))
+        psum_p = ctx.enter_context(tc.psum_pool(name="psum_p", bufs=UNITS))
+        psum_ut = ctx.enter_context(tc.psum_pool(name="psum_ut", bufs=TILES_PER_ROUND))
+        psum_xt = ctx.enter_context(tc.psum_pool(name="psum_xt", bufs=1))
+        psum_y = ctx.enter_context(tc.psum_pool(name="psum_y", bufs=1))
+
+        x_view = x.rearrange("(p t) k -> p t k", t=TILES)
+        bias_view = norm_bias.rearrange("(p t) h d -> p t (h d)", t=TILES)
+        out_view = out.rearrange("(p t) f -> p t f", t=TILES)
+
+        x_rows, bias_rows, bias_scaled = {}, {}, {}
+        xt_banks, x_grouped, x_codes, x_scales = {}, {}, {}, {}
+        p_banks, norms, p_scales, u_rows, ut_banks = {}, {}, {}, {}, {}
+        u_grouped, u_codes, u_scales, y_banks = {}, {}, {}, {}
+
+        def tiles_of(r):
+            return slice(r * TILES_PER_ROUND, (r + 1) * TILES_PER_ROUND)
+
+        def block(i, width):
+            return slice(i * width, (i + 1) * width)
+
+        def load_x(r):
+            rows = loads.tile([P, TILES_PER_ROUND * K_IN], BF16, name="x_rows")
+            nc.sync.dma_start(
+                out=rows[:].rearrange("p (t k) -> p t k", t=TILES_PER_ROUND), in_=x_view[:, tiles_of(r), :]
+            )
+            x_rows[r] = rows
+
+        def load_bias(r):
+            rows = loads.tile([P, UNITS * D_HEAD], BF16, name="bias_rows")
+            nc.sync.dma_start(
+                out=rows[:].rearrange("p (t d) -> p t d", t=TILES_PER_ROUND), in_=bias_view[:, tiles_of(r), :]
+            )
+            bias_rows[r] = rows
+
+        def scale_bias(r):
+            scaled = ring3.tile([P, UNITS * D_HEAD], F32, name="bias_scaled")
+            nc.gpsimd.tensor_scalar(
+                out=scaled[:], in0=bias_rows[r][:], scalar1=1.0 / math.sqrt(2.0), scalar2=0.0, op0=ALU.mult, op1=ALU.add
+            )
+            bias_scaled[r] = scaled
+
+        def transpose_x(r):
+            bank = psum_xt.tile([P, TILES_PER_ROUND, HALVES, P], F32, name="xt_bank")
+            words = x_rows[r][:].bitcast(F32)
+            for t in range(TILES_PER_ROUND):
+                for half in range(HALVES):
+                    nc.tensor.transpose(bank[:, t, half, :], words[:, block(t * HALVES + half, P)], identity[:])
+            xt_banks[r] = bank
+
+        def fetch_x(r):
+            grouped = work.tile([P, TILES_PER_ROUND * P * PACK], BF16, name="x_grouped", align_bytes=64)
+            nc.vector.tensor_copy(
+                out=grouped[:].bitcast(F32).rearrange("p (t r half) -> p t r half", t=TILES_PER_ROUND, half=HALVES),
+                in_=xt_banks[r][:].rearrange("p t half r -> p t r half"),
+            )
+            x_grouped[r] = grouped
+
+        def quantise_x(r):
+            codes = work.tile([P, TILES_PER_ROUND * P], U32, name="x_codes", align_bytes=64)
+            scales = work.tile([P, TILES_PER_ROUND * P], U8, name="x_scales", align_bytes=64)
+            nc.vector.quantize_mx(out=codes[:].bitcast(FP8X4), scales=scales[:], in_=x_grouped[r][:])
+            x_codes[r], x_scales[r] = codes, scales
+
+        def project(r, unit):
+            t, h = divmod(unit, HEADS)
+            bank = psum_p.tile([P, D_HEAD], F32, name="p_bank")
+            nc.tensor.matmul_mx(
+                out=bank[:],
+                lhsT=x_codes[r][:, block(t, P)].bitcast(FP8X4),
+                lhsT_scale=x_scales[r][:, block(t, P)],
+                rhs=w_codes[:, block(h, D_HEAD)].bitcast(FP8X4),
+                rhs_scale=w_scales[:, block(h, D_HEAD)],
+                start=True,
+                stop=True,
+            )
+            p_banks[r, unit] = bank
+
+        def measure(r):
+            sum_sq = ring3.tile([P, UNITS], F32, name="sum_sq")
+            for unit in range(UNITS):
+                squares = ring4.tile([P, D_HEAD], BF16, name="squares")
+                nc.scalar.activation(
+                    out=squares[:], in_=p_banks[r, unit][:], func=ACT.Square, accum_out=sum_sq[:, unit : unit + 1]
+                )
+            norm = ring3.tile([P, UNITS], F32, name="norm")
+            nc.scalar.activation(out=norm[:], in_=sum_sq[:], func=ACT.Sqrt, scale=2.0 / D_HEAD, bias=2.0 * EPSILON)
+            norms[r] = norm
+
+        def invert_norm(r):
+            p_scale = ring3.tile([P, UNITS], F32, name="p_scale")
+            nc.vector.reciprocal(out=p_scale[:], in_=norms[r][:])
+            p_scales[r] = p_scale
+            u_rows[r] = work.tile([P, UNITS * D_HEAD], BF16, name="u_rows")
+
+        def blend(r, unit):
+            nc.vector.scalar_tensor_tensor(
+                out=u_rows[r][:, block(unit, D_HEAD)],
+                in0=p_banks[r, unit][:],
+                scalar=p_scales[r][:, unit : unit + 1],
+                in1=bias_scaled[r][:, block(unit, D_HEAD)],
+                op0=ALU.mult,
+                op1=ALU.add,
+            )
+
+        def transpose_u(r):
+            words = u_rows[r][:].bitcast(F32)
+            for t in range(TILES_PER_ROUND):
+                bank = psum_ut.tile([P, HEADS, HALVES, P], F32, name="ut_bank")
+                for part in range(HEADS * HALVES):
+                    h, half = divmod(part, HALVES)
+                    nc.tensor.transpose(
+                        bank[:, h, half, :], words[:, block(t * HEADS * HALVES + part, P)], identity[:]
+                    )
+                ut_banks[r, t] = bank
+
+        def fetch_u(r):
+            grouped = work.tile([P, UNITS * P * PACK], BF16, name="u_grouped", align_bytes=64)
+            pairs = grouped[:].bitcast(F32).rearrange(
+                "p (t h r half) -> p t h r half", t=TILES_PER_ROUND, h=HEADS, half=HALVES
+            )
+            for t in range(TILES_PER_ROUND):
+                nc.scalar.copy(out=pairs[:, t], in_=ut_banks[r, t][:].rearrange("p h half r -> p h r half"))
+            u_grouped[r] = grouped
+
+        def quantise_u(r):
+            codes = work.tile([P, UNITS * P], U32, name="u_codes", align_bytes=64)
+            scales = work.tile([P, UNITS * P], U8, name="u_scales", align_bytes=64)
+            nc.vector.quantize_mx(out=codes[:].bitcast(FP8X4), scales=scales[:], in_=u_grouped[r][:])
+            u_codes[r], u_scales[r] = codes, scales
+
+        def project_heads(r):
+            bank = psum_y.tile([P, UNITS * F_OUT], F32, name="y_bank")
+            for unit in range(UNITS):
+                h = unit % HEADS
+                nc.tensor.matmul_mx(
+                    out=bank[:, block(unit, F_OUT)],
+                    lhsT=u_codes[r][:, block(unit, P)].bitcast(FP8X4),
+                    lhsT_scale=u_scales[r][:, block(unit, P)],
+                    rhs=k_codes[:, block(h, F_OUT)].bitcast(FP8X4),
+                    rhs_scale=k_scales[:, block(h, F_OUT)],
+                    start=True,
+                    stop=True,
+                )
+            y_banks[r] = bank
+
+        def store_y(r):
+            y_rows = ring4.tile([P, UNITS * F_OUT], F32, name="y_rows")
+            nc.scalar.copy(out=y_rows[:], in_=y_banks[r][:])
+            nc.sync.dma_start(
+                out=out_view[:, tiles_of(r), :], in_=y_rows[:].rearrange("p (t f) -> p t f", t=TILES_PER_ROUND)
+            )
+
+        def load_weights():
+            w_view = w_lin.rearrange("(half q e) c -> half q e c", half=HALVES, e=2)
+            k_view = kernel.rearrange("h (half q e) f -> h half q e f", half=HALVES, e=2)
+            for half in range(HALVES):
+                nc.sync.dma_start(out=w_rows[:, block(half, 2), :], in_=w_view[half])
+            for h in range(HEADS):
+                for half in range(HALVES):
+                    nc.sync.dma_start(out=k_rows[:, h, block(half, 2), :], in_=k_view[h, half])
+
+        def quantise_weights():
+            w_grouped = consts.tile([P, HEADS * D_HEAD, PACK], BF16, name="w_grouped", align_bytes=64)
+            k_grouped = consts.tile([P, HEADS, F_OUT, PACK], BF16, name="k_grouped", align_bytes=64)
+            nc.vector.tensor_copy(
+                out=w_grouped[:, block(0, D_HEAD), :], in_=w_rows[:, :, block(0, D_HEAD)].rearrange("p t c -> p c t")
+            )
+            nc.scalar.copy(
+                out=w_grouped[:, block(1, D_HEAD), :], in_=w_rows[:, :, block(1, D_HEAD)].rearrange("p t c -> p c t")
+            )
+            nc.vector.tensor_copy(out=k_grouped[:], in_=k_rows[:].rearrange("p h t f -> p h f t"))
+            for h in range(HEADS):
+                nc.vector.quantize_mx(
+                    out=w_codes[:, block(h, D_HEAD)].bitcast(FP8X4),
+                    scales=w_scales[:, block(h, D_HEAD)],
+                    in_=w_grouped[:, block(h, D_HEAD), :].rearrange("p c t -> p (c t)"),
+                )
+            nc.vector.quantize_mx(
+                out=k_codes[:].bitcast(FP8X4), scales=k_scales[:], in_=k_grouped[:].rearrange("p h f t -> p (h f t)")
+            )
+
+        def step(s):
+            def live(r):
+                return 0 <= r < ROUNDS
+
+            if live(s + LOAD_AHEAD):
+                load_x(s + LOAD_AHEAD)
+                load_bias(s + LOAD_AHEAD)
+            if live(s - 3):
+                measure(s - 3)
+            if live(s - 4):
+                fetch_u(s - 4)
+            if live(s - LAST_STAGE):
+                store_y(s - LAST_STAGE)
+            if live(s - 3):
+                invert_norm(s - 3)
+            for unit in range(UNITS):
+                if live(s - 3):
+                    blend(s - 3, unit)
+                if live(s - 2):
+                    project(s - 2, unit)
+            if live(s - 3):
+                transpose_u(s - 3)
+            if live(s - 1):
+                fetch_x(s - 1)
+            if live(s):
+                transpose_x(s)
+            if live(s - 4):
+                quantise_u(s - 4)
+            if live(s - 1):
+                quantise_x(s - 1)
+                scale_bias(s - 1)
+            if live(s - 4):
+                project_heads(s - 4)
+
+        w_rows = consts.tile([P, PACK, HEADS * D_HEAD], BF16, name="w_rows")
+        k_rows = consts.tile([P, HEADS, PACK, F_OUT], BF16, name="k_rows")
+        w_codes = consts.tile([P, HEADS * D_HEAD], U32, name="w_codes", align_bytes=64)
+        w_scales = consts.tile([P, HEADS * D_HEAD], U8, name="w_scales", align_bytes=64)
+        k_codes = consts.tile([P, HEADS * F_OUT], U32, name="k_codes", align_bytes=64)
+        k_scales = consts.tile([P, HEADS * F_OUT], U8, name="k_scales", align_bytes=64)
+        identity = consts.tile([P, P], F32, name="identity")
+        one = consts.tile([P, 1], F32, name="one")
+
+        load_x(0)
+        load_weights()
+        load_bias(0)
+        for r in range(1, LOAD_AHEAD):
+            load_x(r)
+            load_bias(r)
+        make_identity(nc, identity[:])
+        nc.vector.memset(one[:], 1.0)
+        nc.scalar.activation(out=one[:], in_=one[:], func=ACT.Sqrt)
+
+        step(0)
+        step(1)
+        quantise_weights()
+        for s in range(2, ROUNDS + LAST_STAGE + 1):
+            step(s)

@@ -77,8 +77,8 @@ def tile_grouplinearblock_pa_t_kernel(tc, x, norm_bias, w_lin, kernel, out):
 
         def scale_bias(r):
             scaled = ring3.tile([P, UNITS * D_HEAD], F32, name="bias_scaled")
-            nc.gpsimd.tensor_scalar(
-                out=scaled[:], in0=bias_rows[r][:], scalar1=1.0 / math.sqrt(2.0), scalar2=0.0, op0=ALU.mult, op1=ALU.add
+            nc.vector.tensor_scalar(
+                out=scaled[:], in0=bias_rows[r][:], scalar1=1.0 / math.sqrt(2.0), scalar2=None, op0=ALU.mult
             )
             bias_scaled[r] = scaled
 

@@ -23,9 +23,8 @@ EPSILON = 1e-06
 
 HALVES = 2
 TILES = TOKENS // P
-TILES_PER_ROUND = 2
-ROUNDS = TILES // TILES_PER_ROUND
-UNITS = TILES_PER_ROUND * HEADS
+PAIR = 2
+ROUNDS = TILES // PAIR
 LOAD_AHEAD = 3
 LAST_STAGE = 5
 
@@ -37,12 +36,10 @@ def tile_grouplinearblock_pa_t_kernel(tc, x, norm_bias, w_lin, kernel, out):
     with ExitStack() as ctx:
         ctx.enter_context(tc.manual_schedule())
         consts = ctx.enter_context(tc.tile_pool(name="consts", bufs=1))
-        loads = ctx.enter_context(tc.tile_pool(name="loads", bufs=LOAD_AHEAD + 3))
-        work = ctx.enter_context(tc.tile_pool(name="work", bufs=2))
-        ring3 = ctx.enter_context(tc.tile_pool(name="ring3", bufs=3))
-        ring4 = ctx.enter_context(tc.tile_pool(name="ring4", bufs=4))
-        psum_p = ctx.enter_context(tc.psum_pool(name="psum_p", bufs=UNITS))
-        psum_ut = ctx.enter_context(tc.psum_pool(name="psum_ut", bufs=TILES_PER_ROUND))
+        loads = ctx.enter_context(tc.tile_pool(name="loads", bufs=LOAD_AHEAD + 4))
+        work = ctx.enter_context(tc.tile_pool(name="work", bufs=4))
+        psum_p = ctx.enter_context(tc.psum_pool(name="psum_p", bufs=HEADS * PAIR))
+        psum_ut = ctx.enter_context(tc.psum_pool(name="psum_ut", bufs=HEADS))
         psum_xt = ctx.enter_context(tc.psum_pool(name="psum_xt", bufs=1))
         psum_y = ctx.enter_context(tc.psum_pool(name="psum_y", bufs=1))
 
@@ -50,62 +47,49 @@ def tile_grouplinearblock_pa_t_kernel(tc, x, norm_bias, w_lin, kernel, out):
         bias_view = norm_bias.rearrange("(p t) h d -> p t (h d)", t=TILES)
         out_view = out.rearrange("(p t) f -> p t f", t=TILES)
 
-        x_rows, bias_rows, bias_scaled = {}, {}, {}
-        xt_banks, x_grouped, x_codes, x_scales = {}, {}, {}, {}
-        p_banks, norms, p_scales, u_rows, ut_banks = {}, {}, {}, {}, {}
-        u_grouped, u_codes, u_scales, y_banks = {}, {}, {}, {}
+        x_rows, bias_rows, xt_banks, x_grouped, x_codes, x_scales, y_banks = {}, {}, {}, {}, {}, {}, {}
+        bias_scaled, p_banks, norms, p_scales, u_rows, ut_banks = {}, {}, {}, {}, {}, {}
+        u_grouped, u_codes, u_scales = {}, {}, {}
 
         def tiles_of(r):
-            return slice(r * TILES_PER_ROUND, (r + 1) * TILES_PER_ROUND)
+            return slice(r * PAIR, (r + 1) * PAIR)
 
         def block(i, width):
             return slice(i * width, (i + 1) * width)
 
         def load_x(r):
-            rows = loads.tile([P, TILES_PER_ROUND * K_IN], BF16, name="x_rows")
-            nc.sync.dma_start(
-                out=rows[:].rearrange("p (t k) -> p t k", t=TILES_PER_ROUND), in_=x_view[:, tiles_of(r), :]
-            )
+            rows = loads.tile([P, PAIR * K_IN], BF16, name="x_rows")
+            nc.sync.dma_start(out=rows[:].rearrange("p (t k) -> p t k", t=PAIR), in_=x_view[:, tiles_of(r), :])
             x_rows[r] = rows
 
         def load_bias(r):
-            rows = loads.tile([P, UNITS * D_HEAD], BF16, name="bias_rows")
-            nc.sync.dma_start(
-                out=rows[:].rearrange("p (t d) -> p t d", t=TILES_PER_ROUND), in_=bias_view[:, tiles_of(r), :]
-            )
+            rows = loads.tile([P, PAIR, HEADS, D_HEAD], BF16, name="bias_rows")
+            nc.sync.dma_start(out=rows[:].rearrange("p t h d -> p t (h d)"), in_=bias_view[:, tiles_of(r), :])
             bias_rows[r] = rows
 
-        def scale_bias(r):
-            scaled = ring3.tile([P, UNITS * D_HEAD], F32, name="bias_scaled")
-            nc.vector.tensor_scalar(
-                out=scaled[:], in0=bias_rows[r][:], scalar1=1.0 / math.sqrt(2.0), scalar2=None, op0=ALU.mult
-            )
-            bias_scaled[r] = scaled
-
         def transpose_x(r):
-            bank = psum_xt.tile([P, TILES_PER_ROUND, HALVES, P], F32, name="xt_bank")
+            bank = psum_xt.tile([P, PAIR, HALVES, P], F32, name="xt_bank")
             words = x_rows[r][:].bitcast(F32)
-            for t in range(TILES_PER_ROUND):
+            for t in range(PAIR):
                 for half in range(HALVES):
                     nc.tensor.transpose(bank[:, t, half, :], words[:, block(t * HALVES + half, P)], identity[:])
             xt_banks[r] = bank
 
         def fetch_x(r):
-            grouped = work.tile([P, TILES_PER_ROUND * P * PACK], BF16, name="x_grouped", align_bytes=64)
-            nc.vector.tensor_copy(
-                out=grouped[:].bitcast(F32).rearrange("p (t r half) -> p t r half", t=TILES_PER_ROUND, half=HALVES),
+            grouped = work.tile([P, PAIR * P * PACK], BF16, name="x_grouped", align_bytes=64)
+            nc.scalar.copy(
+                out=grouped[:].bitcast(F32).rearrange("p (t r half) -> p t r half", t=PAIR, half=HALVES),
                 in_=xt_banks[r][:].rearrange("p t half r -> p t r half"),
             )
             x_grouped[r] = grouped
 
         def quantise_x(r):
-            codes = work.tile([P, TILES_PER_ROUND * P], U32, name="x_codes", align_bytes=64)
-            scales = work.tile([P, TILES_PER_ROUND * P], U8, name="x_scales", align_bytes=64)
+            codes = work.tile([P, PAIR * P], U32, name="x_codes", align_bytes=64)
+            scales = work.tile([P, PAIR * P], U8, name="x_scales", align_bytes=64)
             nc.vector.quantize_mx(out=codes[:].bitcast(FP8X4), scales=scales[:], in_=x_grouped[r][:])
             x_codes[r], x_scales[r] = codes, scales
 
-        def project(r, unit):
-            t, h = divmod(unit, HEADS)
+        def project(r, h, t):
             bank = psum_p.tile([P, D_HEAD], F32, name="p_bank")
             nc.tensor.matmul_mx(
                 out=bank[:],
@@ -116,110 +100,111 @@ def tile_grouplinearblock_pa_t_kernel(tc, x, norm_bias, w_lin, kernel, out):
                 start=True,
                 stop=True,
             )
-            p_banks[r, unit] = bank
+            p_banks[r, h, t] = bank
 
-        def measure(r):
-            sum_sq = ring3.tile([P, UNITS], F32, name="sum_sq")
-            for unit in range(UNITS):
-                squares = ring4.tile([P, D_HEAD], BF16, name="squares")
+        def measure(r, h):
+            sum_sq = work.tile([P, PAIR], F32, name="sum_sq")
+            for t in range(PAIR):
+                squares = work.tile([P, D_HEAD], BF16, name="squares")
                 nc.scalar.activation(
-                    out=squares[:], in_=p_banks[r, unit][:], func=ACT.Square, accum_out=sum_sq[:, unit : unit + 1]
+                    out=squares[:], in_=p_banks[r, h, t][:], func=ACT.Square, accum_out=sum_sq[:, t : t + 1]
                 )
-            norm = ring3.tile([P, UNITS], F32, name="norm")
+            norm = work.tile([P, PAIR], F32, name="norm")
             nc.scalar.activation(out=norm[:], in_=sum_sq[:], func=ACT.Sqrt, scale=2.0 / D_HEAD, bias=2.0 * EPSILON)
-            norms[r] = norm
+            norms[r, h] = norm
 
-        def invert_norm(r):
-            p_scale = ring3.tile([P, UNITS], F32, name="p_scale")
-            nc.vector.reciprocal(out=p_scale[:], in_=norms[r][:])
-            p_scales[r] = p_scale
-            u_rows[r] = work.tile([P, UNITS * D_HEAD], BF16, name="u_rows")
+        def scale_bias(r, h):
+            scaled = work.tile([P, PAIR, D_HEAD], F32, name="bias_scaled")
+            nc.vector.tensor_scalar(
+                out=scaled[:], in0=bias_rows[r][:, :, h, :], scalar1=1.0 / math.sqrt(2.0), scalar2=None, op0=ALU.mult
+            )
+            bias_scaled[r, h] = scaled
 
-        def blend(r, unit):
+        def invert_norm(r, h):
+            p_scale = work.tile([P, PAIR], F32, name="p_scale")
+            nc.vector.reciprocal(out=p_scale[:], in_=norms[r, h][:])
+            p_scales[r, h] = p_scale
+            u_rows[r, h] = work.tile([P, PAIR * D_HEAD], BF16, name="u_rows")
+
+        def blend(r, h, t):
             nc.vector.scalar_tensor_tensor(
-                out=u_rows[r][:, block(unit, D_HEAD)],
-                in0=p_banks[r, unit][:],
-                scalar=p_scales[r][:, unit : unit + 1],
-                in1=bias_scaled[r][:, block(unit, D_HEAD)],
+                out=u_rows[r, h][:, block(t, D_HEAD)],
+                in0=p_banks[r, h, t][:],
+                scalar=p_scales[r, h][:, t : t + 1],
+                in1=bias_scaled[r, h][:, t, :],
                 op0=ALU.mult,
                 op1=ALU.add,
             )
 
-        def transpose_u(r):
-            words = u_rows[r][:].bitcast(F32)
-            for t in range(TILES_PER_ROUND):
-                bank = psum_ut.tile([P, HEADS, HALVES, P], F32, name="ut_bank")
-                for part in range(HEADS * HALVES):
-                    h, half = divmod(part, HALVES)
-                    nc.tensor.transpose(
-                        bank[:, h, half, :], words[:, block(t * HEADS * HALVES + part, P)], identity[:]
-                    )
-                ut_banks[r, t] = bank
+        def transpose_u(r, h):
+            bank = psum_ut.tile([P, PAIR, HALVES, P], F32, name="ut_bank")
+            words = u_rows[r, h][:].bitcast(F32)
+            for t in range(PAIR):
+                for half in range(HALVES):
+                    nc.tensor.transpose(bank[:, t, half, :], words[:, block(t * HALVES + half, P)], identity[:])
+            ut_banks[r, h] = bank
 
-        def fetch_u(r):
-            grouped = work.tile([P, UNITS * P * PACK], BF16, name="u_grouped", align_bytes=64)
-            pairs = grouped[:].bitcast(F32).rearrange(
-                "p (t h r half) -> p t h r half", t=TILES_PER_ROUND, h=HEADS, half=HALVES
+        def fetch_u(r, h):
+            grouped = work.tile([P, PAIR * P * PACK], BF16, name="u_grouped", align_bytes=64)
+            nc.scalar.copy(
+                out=grouped[:].bitcast(F32).rearrange("p (t r half) -> p t r half", t=PAIR, half=HALVES),
+                in_=ut_banks[r, h][:].rearrange("p t half r -> p t r half"),
             )
-            for t in range(TILES_PER_ROUND):
-                nc.scalar.copy(out=pairs[:, t], in_=ut_banks[r, t][:].rearrange("p h half r -> p h r half"))
-            u_grouped[r] = grouped
+            u_grouped[r, h] = grouped
 
-        def quantise_u(r):
-            codes = work.tile([P, UNITS * P], U32, name="u_codes", align_bytes=64)
-            scales = work.tile([P, UNITS * P], U8, name="u_scales", align_bytes=64)
-            nc.vector.quantize_mx(out=codes[:].bitcast(FP8X4), scales=scales[:], in_=u_grouped[r][:])
-            u_codes[r], u_scales[r] = codes, scales
+        def quantise_u(r, h):
+            codes = work.tile([P, PAIR * P], U32, name="u_codes", align_bytes=64)
+            scales = work.tile([P, PAIR * P], U8, name="u_scales", align_bytes=64)
+            nc.vector.quantize_mx(out=codes[:].bitcast(FP8X4), scales=scales[:], in_=u_grouped[r, h][:])
+            u_codes[r, h], u_scales[r, h] = codes, scales
 
         def project_heads(r):
-            bank = psum_y.tile([P, UNITS * F_OUT], F32, name="y_bank")
-            for unit in range(UNITS):
-                h = unit % HEADS
-                nc.tensor.matmul_mx(
-                    out=bank[:, block(unit, F_OUT)],
-                    lhsT=u_codes[r][:, block(unit, P)].bitcast(FP8X4),
-                    lhsT_scale=u_scales[r][:, block(unit, P)],
-                    rhs=k_codes[:, block(h, F_OUT)].bitcast(FP8X4),
-                    rhs_scale=k_scales[:, block(h, F_OUT)],
-                    start=True,
-                    stop=True,
-                )
+            bank = psum_y.tile([P, PAIR, HEADS, F_OUT], F32, name="y_bank")
+            for h in range(HEADS):
+                for t in range(PAIR):
+                    nc.tensor.matmul_mx(
+                        out=bank[:, t, h, :],
+                        lhsT=u_codes[r, h][:, block(t, P)].bitcast(FP8X4),
+                        lhsT_scale=u_scales[r, h][:, block(t, P)],
+                        rhs=k_codes[:, block(h, F_OUT)].bitcast(FP8X4),
+                        rhs_scale=k_scales[:, block(h, F_OUT)],
+                        start=True,
+                        stop=True,
+                    )
             y_banks[r] = bank
 
         def store_y(r):
-            y_rows = ring4.tile([P, UNITS * F_OUT], F32, name="y_rows")
-            nc.scalar.copy(out=y_rows[:], in_=y_banks[r][:])
-            nc.sync.dma_start(
-                out=out_view[:, tiles_of(r), :], in_=y_rows[:].rearrange("p (t f) -> p t f", t=TILES_PER_ROUND)
-            )
+            y_rows = work.tile([P, PAIR, HEADS * F_OUT], F32, name="y_rows")
+            nc.scalar.copy(out=y_rows[:], in_=y_banks[r][:].rearrange("p t h f -> p t (h f)"))
+            nc.sync.dma_start(out=out_view[:, tiles_of(r), :], in_=y_rows[:])
 
-        def load_weights():
+        def load_w(h):
             w_view = w_lin.rearrange("(half q e) c -> half q e c", half=HALVES, e=2)
-            k_view = kernel.rearrange("h (half q e) f -> h half q e f", half=HALVES, e=2)
             for half in range(HALVES):
-                nc.sync.dma_start(out=w_rows[:, block(half, 2), :], in_=w_view[half])
+                nc.sync.dma_start(
+                    out=w_rows[:, block(half, 2), block(h, D_HEAD)], in_=w_view[half][:, :, block(h, D_HEAD)]
+                )
+
+        def load_kernel():
+            k_view = kernel.rearrange("h (half q e) f -> h half q e f", half=HALVES, e=2)
             for h in range(HEADS):
                 for half in range(HALVES):
                     nc.sync.dma_start(out=k_rows[:, h, block(half, 2), :], in_=k_view[h, half])
 
-        def quantise_weights():
-            w_grouped = consts.tile([P, HEADS * D_HEAD, PACK], BF16, name="w_grouped", align_bytes=64)
-            k_grouped = consts.tile([P, HEADS, F_OUT, PACK], BF16, name="k_grouped", align_bytes=64)
-            nc.vector.tensor_copy(
-                out=w_grouped[:, block(0, D_HEAD), :], in_=w_rows[:, :, block(0, D_HEAD)].rearrange("p t c -> p c t")
-            )
-            nc.scalar.copy(
-                out=w_grouped[:, block(1, D_HEAD), :], in_=w_rows[:, :, block(1, D_HEAD)].rearrange("p t c -> p c t")
-            )
-            nc.vector.tensor_copy(out=k_grouped[:], in_=k_rows[:].rearrange("p h t f -> p h f t"))
-            for h in range(HEADS):
-                nc.vector.quantize_mx(
-                    out=w_codes[:, block(h, D_HEAD)].bitcast(FP8X4),
-                    scales=w_scales[:, block(h, D_HEAD)],
-                    in_=w_grouped[:, block(h, D_HEAD), :].rearrange("p c t -> p (c t)"),
-                )
+        def quantise_w(h):
+            grouped = work.tile([P, D_HEAD, PACK], BF16, name="w_grouped", align_bytes=64)
+            nc.vector.tensor_copy(out=grouped[:], in_=w_rows[:, :, block(h, D_HEAD)].rearrange("p t c -> p c t"))
             nc.vector.quantize_mx(
-                out=k_codes[:].bitcast(FP8X4), scales=k_scales[:], in_=k_grouped[:].rearrange("p h f t -> p (h f t)")
+                out=w_codes[:, block(h, D_HEAD)].bitcast(FP8X4),
+                scales=w_scales[:, block(h, D_HEAD)],
+                in_=grouped[:].rearrange("p c t -> p (c t)"),
+            )
+
+        def quantise_kernel():
+            grouped = consts.tile([P, HEADS, F_OUT, PACK], BF16, name="k_grouped", align_bytes=64)
+            nc.vector.tensor_copy(out=grouped[:], in_=k_rows[:].rearrange("p h t f -> p h f t"))
+            nc.vector.quantize_mx(
+                out=k_codes[:].bitcast(FP8X4), scales=k_scales[:], in_=grouped[:].rearrange("p h f t -> p (h f t)")
             )
 
         def step(s):
@@ -229,30 +214,35 @@ def tile_grouplinearblock_pa_t_kernel(tc, x, norm_bias, w_lin, kernel, out):
             if live(s + LOAD_AHEAD):
                 load_x(s + LOAD_AHEAD)
                 load_bias(s + LOAD_AHEAD)
-            if live(s - 3):
-                measure(s - 3)
-            if live(s - 4):
-                fetch_u(s - 4)
+            for h in range(HEADS):
+                if live(s - 3):
+                    measure(s - 3, h)
+            for h in range(HEADS):
+                if live(s - 4):
+                    fetch_u(s - 4, h)
             if live(s - LAST_STAGE):
                 store_y(s - LAST_STAGE)
-            if live(s - 3):
-                invert_norm(s - 3)
-            for unit in range(UNITS):
-                if live(s - 3):
-                    blend(s - 3, unit)
-                if live(s - 2):
-                    project(s - 2, unit)
-            if live(s - 3):
-                transpose_u(s - 3)
             if live(s - 1):
                 fetch_x(s - 1)
+            for h in range(HEADS):
+                if live(s - 3):
+                    scale_bias(s - 3, h)
+                    invert_norm(s - 3, h)
+                for t in range(PAIR):
+                    if live(s - 3):
+                        blend(s - 3, h, t)
+                    if live(s - 2):
+                        project(s - 2, h, t)
+            for h in range(HEADS):
+                if live(s - 3):
+                    transpose_u(s - 3, h)
             if live(s):
                 transpose_x(s)
-            if live(s - 4):
-                quantise_u(s - 4)
+            for h in range(HEADS):
+                if live(s - 4):
+                    quantise_u(s - 4, h)
             if live(s - 1):
                 quantise_x(s - 1)
-                scale_bias(s - 1)
             if live(s - 4):
                 project_heads(s - 4)
 
@@ -266,17 +256,23 @@ def tile_grouplinearblock_pa_t_kernel(tc, x, norm_bias, w_lin, kernel, out):
         one = consts.tile([P, 1], F32, name="one")
 
         load_x(0)
-        load_weights()
+        load_w(0)
+        load_w(1)
         load_bias(0)
         for r in range(1, LOAD_AHEAD):
             load_x(r)
             load_bias(r)
+        load_kernel()
         make_identity(nc, identity[:])
         nc.vector.memset(one[:], 1.0)
         nc.scalar.activation(out=one[:], in_=one[:], func=ACT.Sqrt)
 
         step(0)
         step(1)
-        quantise_weights()
-        for s in range(2, ROUNDS + LAST_STAGE + 1):
+        quantise_w(0)
+        quantise_w(1)
+        step(2)
+        step(3)
+        quantise_kernel()
+        for s in range(4, ROUNDS + LAST_STAGE + 1):
             step(s)

@@ -38,6 +38,7 @@ def tile_grouplinearblock_pa_t_kernel(tc, x, norm_bias, w_lin, kernel, out):
         consts = ctx.enter_context(tc.tile_pool(name="consts", bufs=1))
         loads = ctx.enter_context(tc.tile_pool(name="loads", bufs=LOAD_AHEAD + 4))
         work = ctx.enter_context(tc.tile_pool(name="work", bufs=4))
+        paced = ctx.enter_context(tc.tile_pool(name="paced", bufs=2))
         psum_p = ctx.enter_context(tc.psum_pool(name="psum_p", bufs=HEADS * PAIR))
         psum_ut = ctx.enter_context(tc.psum_pool(name="psum_ut", bufs=HEADS))
         psum_xt = ctx.enter_context(tc.psum_pool(name="psum_xt", bufs=1))
@@ -77,7 +78,7 @@ def tile_grouplinearblock_pa_t_kernel(tc, x, norm_bias, w_lin, kernel, out):
 
         def fetch_x(r):
             grouped = work.tile([P, PAIR * P * PACK], BF16, name="x_grouped", align_bytes=64)
-            nc.scalar.copy(
+            nc.vector.tensor_copy(
                 out=grouped[:].bitcast(F32).rearrange("p (t r half) -> p t r half", t=PAIR, half=HALVES),
                 in_=xt_banks[r][:].rearrange("p t half r -> p t r half"),
             )
@@ -113,10 +114,15 @@ def tile_grouplinearblock_pa_t_kernel(tc, x, norm_bias, w_lin, kernel, out):
             nc.scalar.activation(out=norm[:], in_=sum_sq[:], func=ACT.Sqrt, scale=2.0 / D_HEAD, bias=2.0 * EPSILON)
             norms[r, h] = norm
 
-        def scale_bias(r, h):
-            scaled = work.tile([P, PAIR, D_HEAD], F32, name="bias_scaled")
-            nc.vector.tensor_scalar(
-                out=scaled[:], in0=bias_rows[r][:, :, h, :], scalar1=1.0 / math.sqrt(2.0), scalar2=None, op0=ALU.mult
+        def scale_bias(engine, pool, r, h):
+            scaled = pool.tile([P, PAIR, D_HEAD], F32, name="bias_scaled")
+            engine.tensor_scalar(
+                out=scaled[:],
+                in0=bias_rows[r][:, :, h, :],
+                scalar1=1.0 / math.sqrt(2.0),
+                scalar2=0.0,
+                op0=ALU.mult,
+                op1=ALU.add,
             )
             bias_scaled[r, h] = scaled
 
@@ -222,17 +228,18 @@ def tile_grouplinearblock_pa_t_kernel(tc, x, norm_bias, w_lin, kernel, out):
                     fetch_u(s - 4, h)
             if live(s - LAST_STAGE):
                 store_y(s - LAST_STAGE)
-            if live(s - 1):
-                fetch_x(s - 1)
             for h in range(HEADS):
                 if live(s - 3):
-                    scale_bias(s - 3, h)
                     invert_norm(s - 3, h)
                 for t in range(PAIR):
                     if live(s - 3):
                         blend(s - 3, h, t)
                     if live(s - 2):
                         project(s - 2, h, t)
+                if h == 0 and live(s - 1):
+                    scale_bias(nc.gpsimd, paced, s - 1, 0)
+            if live(s - 1):
+                fetch_x(s - 1)
             for h in range(HEADS):
                 if live(s - 3):
                     transpose_u(s - 3, h)
@@ -243,6 +250,8 @@ def tile_grouplinearblock_pa_t_kernel(tc, x, norm_bias, w_lin, kernel, out):
                     quantise_u(s - 4, h)
             if live(s - 1):
                 quantise_x(s - 1)
+            if live(s - 2):
+                scale_bias(nc.vector, work, s - 2, 1)
             if live(s - 4):
                 project_heads(s - 4)
 

@@ -49,7 +49,7 @@ def tile_grouplinearblock_pa_t_kernel(tc, x, norm_bias, w_lin, kernel, out):
         out_view = out.rearrange("(p t) f -> p t f", t=TILES)
 
         x_rows, bias_rows, xt_banks, x_grouped, x_codes, x_scales, y_banks = {}, {}, {}, {}, {}, {}, {}
-        bias_scaled, p_banks, norms, p_scales, u_rows, ut_banks = {}, {}, {}, {}, {}, {}
+        bias_scaled, p_banks, sums_sq, p_scales, u_rows, ut_banks = {}, {}, {}, {}, {}, {}
         u_grouped, u_codes, u_scales = {}, {}, {}
 
         def tiles_of(r):
@@ -103,16 +103,24 @@ def tile_grouplinearblock_pa_t_kernel(tc, x, norm_bias, w_lin, kernel, out):
             )
             p_banks[r, h, t] = bank
 
-        def measure(r, h):
-            sum_sq = work.tile([P, PAIR], F32, name="sum_sq")
-            for t in range(PAIR):
-                squares = work.tile([P, D_HEAD], BF16, name="squares")
-                nc.scalar.activation(
-                    out=squares[:], in_=p_banks[r, h, t][:], func=ACT.Square, accum_out=sum_sq[:, t : t + 1]
-                )
-            norm = work.tile([P, PAIR], F32, name="norm")
-            nc.scalar.activation(out=norm[:], in_=sum_sq[:], func=ACT.Sqrt, scale=2.0 / D_HEAD, bias=2.0 * EPSILON)
-            norms[r, h] = norm
+        def sum_squares(r, h, t):
+            if t == 0:
+                sums_sq[r, h] = work.tile([P, PAIR], F32, name="sum_sq")
+            squares = work.tile([P, D_HEAD], BF16, name="squares")
+            nc.scalar.activation(
+                out=squares[:], in_=p_banks[r, h, t][:], func=ACT.Square, accum_out=sums_sq[r, h][:, t : t + 1]
+            )
+
+        def scale_of_p(r, h):
+            p_scale = work.tile([P, PAIR], F32, name="p_scale")
+            nc.scalar.activation(
+                out=p_scale[:],
+                in_=sums_sq[r, h][:],
+                func=ACT.Abs_reciprocal_sqrt,
+                scale=2.0 / D_HEAD,
+                bias=2.0 * EPSILON,
+            )
+            p_scales[r, h] = p_scale
 
         def scale_bias(engine, pool, r, h):
             scaled = pool.tile([P, PAIR, D_HEAD], F32, name="bias_scaled")
@@ -126,13 +134,9 @@ def tile_grouplinearblock_pa_t_kernel(tc, x, norm_bias, w_lin, kernel, out):
             )
             bias_scaled[r, h] = scaled
 
-        def invert_norm(r, h):
-            p_scale = work.tile([P, PAIR], F32, name="p_scale")
-            nc.vector.reciprocal(out=p_scale[:], in_=norms[r, h][:])
-            p_scales[r, h] = p_scale
-            u_rows[r, h] = work.tile([P, PAIR * D_HEAD], BF16, name="u_rows")
-
         def blend(r, h, t):
+            if t == 0:
+                u_rows[r, h] = work.tile([P, PAIR * D_HEAD], BF16, name="u_rows")
             nc.vector.scalar_tensor_tensor(
                 out=u_rows[r, h][:, block(t, D_HEAD)],
                 in0=p_banks[r, h, t][:],
@@ -151,18 +155,20 @@ def tile_grouplinearblock_pa_t_kernel(tc, x, norm_bias, w_lin, kernel, out):
             ut_banks[r, h] = bank
 
         def fetch_u(r, h):
-            grouped = work.tile([P, PAIR * P * PACK], BF16, name="u_grouped", align_bytes=64)
+            if h == 0:
+                u_grouped[r] = work.tile([P, HEADS * PAIR * P * PACK], BF16, name="u_grouped", align_bytes=64)
             nc.scalar.copy(
-                out=grouped[:].bitcast(F32).rearrange("p (t r half) -> p t r half", t=PAIR, half=HALVES),
+                out=u_grouped[r][:]
+                .bitcast(F32)[:, block(h, PAIR * P * HALVES)]
+                .rearrange("p (t r half) -> p t r half", t=PAIR, half=HALVES),
                 in_=ut_banks[r, h][:].rearrange("p t half r -> p t r half"),
             )
-            u_grouped[r, h] = grouped
 
-        def quantise_u(r, h):
-            codes = work.tile([P, PAIR * P], U32, name="u_codes", align_bytes=64)
-            scales = work.tile([P, PAIR * P], U8, name="u_scales", align_bytes=64)
-            nc.vector.quantize_mx(out=codes[:].bitcast(FP8X4), scales=scales[:], in_=u_grouped[r, h][:])
-            u_codes[r, h], u_scales[r, h] = codes, scales
+        def quantise_u(r):
+            codes = work.tile([P, HEADS * PAIR * P], U32, name="u_codes", align_bytes=64)
+            scales = work.tile([P, HEADS * PAIR * P], U8, name="u_scales", align_bytes=64)
+            nc.vector.quantize_mx(out=codes[:].bitcast(FP8X4), scales=scales[:], in_=u_grouped[r][:])
+            u_codes[r], u_scales[r] = codes, scales
 
         def project_heads(r):
             bank = psum_y.tile([P, PAIR, HEADS, F_OUT], F32, name="y_bank")
@@ -170,8 +176,8 @@ def tile_grouplinearblock_pa_t_kernel(tc, x, norm_bias, w_lin, kernel, out):
                 for t in range(PAIR):
                     nc.tensor.matmul_mx(
                         out=bank[:, t, h, :],
-                        lhsT=u_codes[r, h][:, block(t, P)].bitcast(FP8X4),
-                        lhsT_scale=u_scales[r, h][:, block(t, P)],
+                        lhsT=u_codes[r][:, block(h * PAIR + t, P)].bitcast(FP8X4),
+                        lhsT_scale=u_scales[r][:, block(h * PAIR + t, P)],
                         rhs=k_codes[:, block(h, F_OUT)].bitcast(FP8X4),
                         rhs_scale=k_scales[:, block(h, F_OUT)],
                         start=True,
@@ -220,17 +226,21 @@ def tile_grouplinearblock_pa_t_kernel(tc, x, norm_bias, w_lin, kernel, out):
             if live(s + LOAD_AHEAD):
                 load_x(s + LOAD_AHEAD)
                 load_bias(s + LOAD_AHEAD)
-            for h in range(HEADS):
-                if live(s - 3):
-                    measure(s - 3, h)
-            for h in range(HEADS):
-                if live(s - 4):
-                    fetch_u(s - 4, h)
+            if live(s - 3):
+                sum_squares(s - 3, 0, 0)
+                sum_squares(s - 3, 0, 1)
+                sum_squares(s - 3, 1, 0)
+                scale_of_p(s - 3, 0)
+                sum_squares(s - 3, 1, 1)
+            if live(s - 4):
+                fetch_u(s - 4, 0)
+            if live(s - 3):
+                scale_of_p(s - 3, 1)
+            if live(s - 4):
+                fetch_u(s - 4, 1)
             if live(s - LAST_STAGE):
                 store_y(s - LAST_STAGE)
             for h in range(HEADS):
-                if live(s - 3):
-                    invert_norm(s - 3, h)
                 for t in range(PAIR):
                     if live(s - 3):
                         blend(s - 3, h, t)
@@ -238,16 +248,14 @@ def tile_grouplinearblock_pa_t_kernel(tc, x, norm_bias, w_lin, kernel, out):
                         project(s - 2, h, t)
                 if h == 0 and live(s - 1):
                     scale_bias(nc.gpsimd, paced, s - 1, 0)
-            if live(s - 1):
-                fetch_x(s - 1)
+                    fetch_x(s - 1)
             for h in range(HEADS):
                 if live(s - 3):
                     transpose_u(s - 3, h)
             if live(s):
                 transpose_x(s)
-            for h in range(HEADS):
-                if live(s - 4):
-                    quantise_u(s - 4, h)
+            if live(s - 4):
+                quantise_u(s - 4)
             if live(s - 1):
                 quantise_x(s - 1)
             if live(s - 2):
@@ -274,7 +282,7 @@ def tile_grouplinearblock_pa_t_kernel(tc, x, norm_bias, w_lin, kernel, out):
         load_kernel()
         make_identity(nc, identity[:])
         nc.vector.memset(one[:], 1.0)
-        nc.scalar.activation(out=one[:], in_=one[:], func=ACT.Sqrt)
+        nc.scalar.activation(out=one[:], in_=one[:], func=ACT.Abs_reciprocal_sqrt)
 
         step(0)
         step(1)

@@ -25,8 +25,9 @@ HALVES = 2
 TILES = TOKENS // P
 PAIR = 2
 ROUNDS = TILES // PAIR
-LOAD_AHEAD = 3
-LAST_STAGE = 5
+LOAD_AHEAD = 6
+TURNS = 3
+W_SPLIT = 336
 
 FLOPS = 2 * TOKENS * K_IN * HEADS * D_HEAD + 2 * TOKENS * HEADS * D_HEAD * F_OUT
 
@@ -36,9 +37,9 @@ def tile_grouplinearblock_pa_t_kernel(tc, x, norm_bias, w_lin, kernel, out):
     with ExitStack() as ctx:
         ctx.enter_context(tc.manual_schedule())
         consts = ctx.enter_context(tc.tile_pool(name="consts", bufs=1))
-        loads = ctx.enter_context(tc.tile_pool(name="loads", bufs=LOAD_AHEAD + 4))
+        loads = ctx.enter_context(tc.tile_pool(name="loads", bufs=LOAD_AHEAD + 2))
         work = ctx.enter_context(tc.tile_pool(name="work", bufs=4))
-        paced = ctx.enter_context(tc.tile_pool(name="paced", bufs=2))
+        turns = ctx.enter_context(tc.tile_pool(name="turns", bufs=1))
         psum_p = ctx.enter_context(tc.psum_pool(name="psum_p", bufs=HEADS * PAIR))
         psum_ut = ctx.enter_context(tc.psum_pool(name="psum_ut", bufs=HEADS))
         psum_xt = ctx.enter_context(tc.psum_pool(name="psum_xt", bufs=1))
@@ -49,8 +50,12 @@ def tile_grouplinearblock_pa_t_kernel(tc, x, norm_bias, w_lin, kernel, out):
         out_view = out.rearrange("(p t) f -> p t f", t=TILES)
 
         x_rows, bias_rows, xt_banks, x_grouped, x_codes, x_scales, y_banks = {}, {}, {}, {}, {}, {}, {}
+        w_grouped = {}
         bias_scaled, p_banks, sums_sq, p_scales, u_rows, ut_banks = {}, {}, {}, {}, {}, {}
-        u_grouped, u_codes, u_scales = {}, {}, {}
+        u_grouped, u_codes, u_scales, y_rows = {}, {}, {}, {}
+
+        def turn_of(r):
+            return "turn%d" % (r % TURNS)
 
         def tiles_of(r):
             return slice(r * PAIR, (r + 1) * PAIR)
@@ -76,9 +81,9 @@ def tile_grouplinearblock_pa_t_kernel(tc, x, norm_bias, w_lin, kernel, out):
                     nc.tensor.transpose(bank[:, t, half, :], words[:, block(t * HALVES + half, P)], identity[:])
             xt_banks[r] = bank
 
-        def fetch_x(r):
-            grouped = work.tile([P, PAIR * P * PACK], BF16, name="x_grouped", align_bytes=64)
-            nc.vector.tensor_copy(
+        def fetch_x(r, copy):
+            grouped = turns.tile([P, PAIR * P * PACK], BF16, name="x_grouped", tag=turn_of(r), align_bytes=64)
+            copy(
                 out=grouped[:].bitcast(F32).rearrange("p (t r half) -> p t r half", t=PAIR, half=HALVES),
                 in_=xt_banks[r][:].rearrange("p t half r -> p t r half"),
             )
@@ -122,17 +127,18 @@ def tile_grouplinearblock_pa_t_kernel(tc, x, norm_bias, w_lin, kernel, out):
             )
             p_scales[r, h] = p_scale
 
-        def scale_bias(engine, pool, r, h):
-            scaled = pool.tile([P, PAIR, D_HEAD], F32, name="bias_scaled")
-            engine.tensor_scalar(
-                out=scaled[:],
-                in0=bias_rows[r][:, :, h, :],
-                scalar1=1.0 / math.sqrt(2.0),
-                scalar2=0.0,
-                op0=ALU.mult,
-                op1=ALU.add,
-            )
-            bias_scaled[r, h] = scaled
+        def scale_bias(r, parts):
+            scaled = turns.tile([P, PAIR, HEADS, D_HEAD], F32, name="bias_scaled", tag=turn_of(r), align_bytes=64)
+            for engine, heads in parts:
+                engine.tensor_scalar(
+                    out=scaled[:, :, heads, :],
+                    in0=bias_rows[r][:, :, heads, :],
+                    scalar1=1.0 / math.sqrt(2.0),
+                    scalar2=0.0,
+                    op0=ALU.mult,
+                    op1=ALU.add,
+                )
+            bias_scaled[r] = scaled
 
         def blend(r, h, t):
             if t == 0:
@@ -141,7 +147,7 @@ def tile_grouplinearblock_pa_t_kernel(tc, x, norm_bias, w_lin, kernel, out):
                 out=u_rows[r, h][:, block(t, D_HEAD)],
                 in0=p_banks[r, h, t][:],
                 scalar=p_scales[r, h][:, t : t + 1],
-                in1=bias_scaled[r, h][:, t, :],
+                in1=bias_scaled[r][:, t, h, :],
                 op0=ALU.mult,
                 op1=ALU.add,
             )
@@ -154,47 +160,58 @@ def tile_grouplinearblock_pa_t_kernel(tc, x, norm_bias, w_lin, kernel, out):
                     nc.tensor.transpose(bank[:, t, half, :], words[:, block(t * HALVES + half, P)], identity[:])
             ut_banks[r, h] = bank
 
-        def fetch_u(r, h):
+        def fetch_u(r, h, copy):
             if h == 0:
                 u_grouped[r] = work.tile([P, HEADS * PAIR * P * PACK], BF16, name="u_grouped", align_bytes=64)
-            nc.scalar.copy(
+            copy(
                 out=u_grouped[r][:]
                 .bitcast(F32)[:, block(h, PAIR * P * HALVES)]
                 .rearrange("p (t r half) -> p t r half", t=PAIR, half=HALVES),
                 in_=ut_banks[r, h][:].rearrange("p t half r -> p t r half"),
             )
 
-        def quantise_u(r):
-            codes = work.tile([P, HEADS * PAIR * P], U32, name="u_codes", align_bytes=64)
-            scales = work.tile([P, HEADS * PAIR * P], U8, name="u_scales", align_bytes=64)
-            nc.vector.quantize_mx(out=codes[:].bitcast(FP8X4), scales=scales[:], in_=u_grouped[r][:])
-            u_codes[r], u_scales[r] = codes, scales
+        def quantise_u(r, part, parts):
+            if part == 0:
+                u_codes[r] = work.tile([P, HEADS * PAIR * P], U32, name="u_codes", align_bytes=64)
+                u_scales[r] = work.tile([P, HEADS * PAIR * P], U8, name="u_scales", align_bytes=64)
+            words = block(part, HEADS * PAIR * P // parts)
+            nc.vector.quantize_mx(
+                out=u_codes[r][:, words].bitcast(FP8X4),
+                scales=u_scales[r][:, words],
+                in_=u_grouped[r][:, block(part, HEADS * PAIR * P * PACK // parts)],
+            )
+
+        def project_head(r, h, bank):
+            for t in range(PAIR):
+                nc.tensor.matmul_mx(
+                    out=bank[:, t, h, :],
+                    lhsT=u_codes[r][:, block(h * PAIR + t, P)].bitcast(FP8X4),
+                    lhsT_scale=u_scales[r][:, block(h * PAIR + t, P)],
+                    rhs=k_codes[:, block(h, F_OUT)].bitcast(FP8X4),
+                    rhs_scale=k_scales[:, block(h, F_OUT)],
+                    start=True,
+                    stop=True,
+                )
 
         def project_heads(r):
             bank = psum_y.tile([P, PAIR, HEADS, F_OUT], F32, name="y_bank")
             for h in range(HEADS):
-                for t in range(PAIR):
-                    nc.tensor.matmul_mx(
-                        out=bank[:, t, h, :],
-                        lhsT=u_codes[r][:, block(h * PAIR + t, P)].bitcast(FP8X4),
-                        lhsT_scale=u_scales[r][:, block(h * PAIR + t, P)],
-                        rhs=k_codes[:, block(h, F_OUT)].bitcast(FP8X4),
-                        rhs_scale=k_scales[:, block(h, F_OUT)],
-                        start=True,
-                        stop=True,
-                    )
+                project_head(r, h, bank)
             y_banks[r] = bank
 
+        def fetch_y(r, t, copy):
+            if t == 0:
+                y_rows[r] = work.tile([P, PAIR, HEADS * F_OUT], F32, name="y_rows")
+            copy(out=y_rows[r][:, t, :], in_=y_banks[r][:, t, :, :].rearrange("p h f -> p (h f)"))
+
         def store_y(r):
-            y_rows = work.tile([P, PAIR, HEADS * F_OUT], F32, name="y_rows")
-            nc.scalar.copy(out=y_rows[:], in_=y_banks[r][:].rearrange("p t h f -> p t (h f)"))
-            nc.sync.dma_start(out=out_view[:, tiles_of(r), :], in_=y_rows[:])
+            nc.sync.dma_start(out=out_view[:, tiles_of(r), :], in_=y_rows[r][:])
 
         def load_w(h):
             w_view = w_lin.rearrange("(half q e) c -> half q e c", half=HALVES, e=2)
             for half in range(HALVES):
                 nc.sync.dma_start(
-                    out=w_rows[:, block(half, 2), block(h, D_HEAD)], in_=w_view[half][:, :, block(h, D_HEAD)]
+                    out=w_rows[h][:, block(half, 2), :], in_=w_view[half][:, :, block(h, D_HEAD)]
                 )
 
         def load_kernel():
@@ -203,13 +220,22 @@ def tile_grouplinearblock_pa_t_kernel(tc, x, norm_bias, w_lin, kernel, out):
                 for half in range(HALVES):
                     nc.sync.dma_start(out=k_rows[:, h, block(half, 2), :], in_=k_view[h, half])
 
+        def group_w(h):
+            w_grouped[h] = consts.tile([P, D_HEAD, PACK], BF16, name="w_grouped%d" % h, align_bytes=64)
+            for copy, columns in (
+                (nc.vector.tensor_copy, slice(0, W_SPLIT)),
+                (nc.scalar.copy, slice(W_SPLIT, D_HEAD)),
+            ):
+                copy(
+                    out=w_grouped[h][:, columns, :].rearrange("p (c i) t -> p c t i", i=4),
+                    in_=w_rows[h][:, :, columns].rearrange("p t (c i) -> p c t i", i=4),
+                )
+
         def quantise_w(h):
-            grouped = work.tile([P, D_HEAD, PACK], BF16, name="w_grouped", align_bytes=64)
-            nc.vector.tensor_copy(out=grouped[:], in_=w_rows[:, :, block(h, D_HEAD)].rearrange("p t c -> p c t"))
             nc.vector.quantize_mx(
                 out=w_codes[:, block(h, D_HEAD)].bitcast(FP8X4),
                 scales=w_scales[:, block(h, D_HEAD)],
-                in_=grouped[:].rearrange("p c t -> p (c t)"),
+                in_=w_grouped[h][:].rearrange("p c t -> p (c t)"),
             )
 
         def quantise_kernel():
@@ -219,51 +245,53 @@ def tile_grouplinearblock_pa_t_kernel(tc, x, norm_bias, w_lin, kernel, out):
                 out=k_codes[:].bitcast(FP8X4), scales=k_scales[:], in_=grouped[:].rearrange("p h f t -> p (h f t)")
             )
 
-        def step(s):
-            def live(r):
-                return 0 <= r < ROUNDS
+        def step(r):
+            def live(i):
+                return 0 <= i < ROUNDS
 
-            if live(s + LOAD_AHEAD):
-                load_x(s + LOAD_AHEAD)
-                load_bias(s + LOAD_AHEAD)
-            if live(s - 3):
-                sum_squares(s - 3, 0, 0)
-                sum_squares(s - 3, 0, 1)
-                sum_squares(s - 3, 1, 0)
-                scale_of_p(s - 3, 0)
-                sum_squares(s - 3, 1, 1)
-            if live(s - 4):
-                fetch_u(s - 4, 0)
-            if live(s - 3):
-                scale_of_p(s - 3, 1)
-            if live(s - 4):
-                fetch_u(s - 4, 1)
-            if live(s - LAST_STAGE):
-                store_y(s - LAST_STAGE)
+            if live(r + LOAD_AHEAD):
+                load_x(r + LOAD_AHEAD)
+                load_bias(r + LOAD_AHEAD)
+            sum_squares(r, 0, 0)
+            sum_squares(r, 0, 1)
+            sum_squares(r, 1, 0)
+            scale_of_p(r, 0)
+            sum_squares(r, 1, 1)
+            if live(r - 1):
+                fetch_u(r - 1, 0, nc.scalar.copy)
+            scale_of_p(r, 1)
+            if live(r - 1):
+                fetch_u(r - 1, 1, nc.scalar.copy)
+            if live(r - 2):
+                fetch_y(r - 2, 0, nc.scalar.copy)
             for h in range(HEADS):
                 for t in range(PAIR):
-                    if live(s - 3):
-                        blend(s - 3, h, t)
-                    if live(s - 2):
-                        project(s - 2, h, t)
-                if h == 0 and live(s - 1):
-                    scale_bias(nc.gpsimd, paced, s - 1, 0)
-                    fetch_x(s - 1)
+                    blend(r, h, t)
+                    if live(r + 1):
+                        project(r + 1, h, t)
+                if h == 0 and live(r + 2):
+                    fetch_x(r + 2, nc.vector.tensor_copy)
+                if h == 1 and live(r - 2):
+                    fetch_y(r - 2, 1, nc.vector.tensor_copy)
+                    store_y(r - 2)
+            if live(r + 1):
+                scale_bias(r + 1, [(nc.gpsimd, slice(0, HEADS))])
             for h in range(HEADS):
-                if live(s - 3):
-                    transpose_u(s - 3, h)
-            if live(s):
-                transpose_x(s)
-            if live(s - 4):
-                quantise_u(s - 4)
-            if live(s - 1):
-                quantise_x(s - 1)
-            if live(s - 2):
-                scale_bias(nc.vector, work, s - 2, 1)
-            if live(s - 4):
-                project_heads(s - 4)
+                transpose_u(r, h)
+            if live(r + 3):
+                transpose_x(r + 3)
+            if live(r - 1):
+                quantise_u(r - 1, 0, 1)
+            else:
+                quantise_kernel()
+            if live(r + 2):
+                quantise_x(r + 2)
+            if live(r - 1):
+                project_heads(r - 1)
 
-        w_rows = consts.tile([P, PACK, HEADS * D_HEAD], BF16, name="w_rows")
+        w_rows = {}
+        for h in range(HEADS):
+            w_rows[h] = consts.tile([P, PACK, D_HEAD], BF16, name="w_rows%d" % h)
         k_rows = consts.tile([P, HEADS, PACK, F_OUT], BF16, name="k_rows")
         w_codes = consts.tile([P, HEADS * D_HEAD], U32, name="w_codes", align_bytes=64)
         w_scales = consts.tile([P, HEADS * D_HEAD], U8, name="w_scales", align_bytes=64)
@@ -272,24 +300,49 @@ def tile_grouplinearblock_pa_t_kernel(tc, x, norm_bias, w_lin, kernel, out):
         identity = consts.tile([P, P], F32, name="identity")
         one = consts.tile([P, 1], F32, name="one")
 
-        load_x(0)
         load_w(0)
+        load_x(0)
+        load_x(1)
         load_w(1)
         load_bias(0)
-        for r in range(1, LOAD_AHEAD):
-            load_x(r)
-            load_bias(r)
+        load_x(2)
+        load_bias(1)
+        load_x(3)
         load_kernel()
+        for r in range(2, LOAD_AHEAD):
+            load_bias(r)
+            if r + 2 < LOAD_AHEAD:
+                load_x(r + 2)
         make_identity(nc, identity[:])
         nc.vector.memset(one[:], 1.0)
         nc.scalar.activation(out=one[:], in_=one[:], func=ACT.Abs_reciprocal_sqrt)
 
-        step(0)
-        step(1)
+        group_w(0)
+        transpose_x(0)
+        fetch_x(0, nc.scalar.copy)
         quantise_w(0)
+        transpose_x(1)
+        fetch_x(1, nc.scalar.copy)
+        quantise_x(0)
+        for t in range(PAIR):
+            project(0, 0, t)
+        group_w(1)
         quantise_w(1)
-        step(2)
-        step(3)
-        quantise_kernel()
-        for s in range(4, ROUNDS + LAST_STAGE + 1):
-            step(s)
+        for t in range(PAIR):
+            project(0, 1, t)
+        transpose_x(2)
+        scale_bias(0, [(nc.vector, slice(0, 1)), (nc.vector, slice(1, 2))])
+        quantise_x(1)
+        for r in range(ROUNDS):
+            step(r)
+        last = ROUNDS - 1
+        fetch_u(last, 0, nc.scalar.copy)
+        fetch_u(last, 1, nc.vector.tensor_copy)
+        fetch_y(last - 1, 0, nc.scalar.copy)
+        fetch_y(last - 1, 1, nc.vector.tensor_copy)
+        store_y(last - 1)
+        quantise_u(last, 0, 1)
+        project_heads(last)
+        fetch_y(last, 0, nc.scalar.copy)
+        fetch_y(last, 1, nc.vector.tensor_copy)
+        store_y(last)

@@ -27,7 +27,7 @@ PAIR = 2
 ROUNDS = TILES // PAIR
 LOAD_AHEAD = 6
 TURNS = 3
-W_SPLIT = 336
+W_SPLIT = (384, 336)
 
 FLOPS = 2 * TOKENS * K_IN * HEADS * D_HEAD + 2 * TOKENS * HEADS * D_HEAD * F_OUT
 
@@ -49,10 +49,14 @@ def tile_grouplinearblock_pa_t_kernel(tc, x, norm_bias, w_lin, kernel, out):
         bias_view = norm_bias.rearrange("(p t) h d -> p t (h d)", t=TILES)
         out_view = out.rearrange("(p t) f -> p t f", t=TILES)
 
-        x_rows, bias_rows, xt_banks, x_grouped, x_codes, x_scales, y_banks = {}, {}, {}, {}, {}, {}, {}
-        w_grouped = {}
+        x_rows, bias_rows, xt_banks, x_grouped, x_codes, x_scales, w_grouped = {}, {}, {}, {}, {}, {}, {}
         bias_scaled, p_banks, sums_sq, p_scales, u_rows, ut_banks = {}, {}, {}, {}, {}, {}
-        u_grouped, u_codes, u_scales, y_rows = {}, {}, {}, {}
+        u_grouped, u_codes, u_scales, y_banks, y_rows = {}, {}, {}, {}, {}
+
+        def parts_of(r):
+            if r == 0:
+                return [(t, h) for h in range(HEADS) for t in range(PAIR)]
+            return [(t, h) for t in range(PAIR) for h in range(HEADS)]
 
         def turn_of(r):
             return "turn%d" % (r % TURNS)
@@ -73,8 +77,8 @@ def tile_grouplinearblock_pa_t_kernel(tc, x, norm_bias, w_lin, kernel, out):
             nc.sync.dma_start(out=rows[:].rearrange("p t h d -> p t (h d)"), in_=bias_view[:, tiles_of(r), :])
             bias_rows[r] = rows
 
-        def transpose_x(r):
-            bank = psum_xt.tile([P, PAIR, HALVES, P], F32, name="xt_bank")
+        def transpose_x(r, pool, tag):
+            bank = pool.tile([P, PAIR, HALVES, P], F32, name="xt_bank", tag=tag)
             words = x_rows[r][:].bitcast(F32)
             for t in range(PAIR):
                 for half in range(HALVES):
@@ -95,8 +99,9 @@ def tile_grouplinearblock_pa_t_kernel(tc, x, norm_bias, w_lin, kernel, out):
             nc.vector.quantize_mx(out=codes[:].bitcast(FP8X4), scales=scales[:], in_=x_grouped[r][:])
             x_codes[r], x_scales[r] = codes, scales
 
-        def project(r, h, t):
-            bank = psum_p.tile([P, D_HEAD], F32, name="p_bank")
+        def project(r, j):
+            t, h = parts_of(r)[j]
+            bank = psum_p.tile([P, D_HEAD], F32, name="p_bank", tag="p_bank")
             nc.tensor.matmul_mx(
                 out=bank[:],
                 lhsT=x_codes[r][:, block(t, P)].bitcast(FP8X4),
@@ -106,103 +111,113 @@ def tile_grouplinearblock_pa_t_kernel(tc, x, norm_bias, w_lin, kernel, out):
                 start=True,
                 stop=True,
             )
-            p_banks[r, h, t] = bank
+            p_banks[r, j] = bank
 
-        def sum_squares(r, h, t):
-            if t == 0:
-                sums_sq[r, h] = work.tile([P, PAIR], F32, name="sum_sq")
+        def sum_squares(r, j):
+            i = j // 2
+            if j % 2 == 0:
+                sums_sq[r, i] = work.tile([P, 2], F32, name="sum_sq")
             squares = work.tile([P, D_HEAD], BF16, name="squares")
             nc.scalar.activation(
-                out=squares[:], in_=p_banks[r, h, t][:], func=ACT.Square, accum_out=sums_sq[r, h][:, t : t + 1]
+                out=squares[:], in_=p_banks[r, j][:], func=ACT.Square, accum_out=sums_sq[r, i][:, j % 2 : j % 2 + 1]
             )
 
-        def scale_of_p(r, h):
-            p_scale = work.tile([P, PAIR], F32, name="p_scale")
+        def scale_of_p(r, i):
+            p_scale = work.tile([P, 2], F32, name="p_scale")
             nc.scalar.activation(
                 out=p_scale[:],
-                in_=sums_sq[r, h][:],
+                in_=sums_sq[r, i][:],
                 func=ACT.Abs_reciprocal_sqrt,
                 scale=2.0 / D_HEAD,
                 bias=2.0 * EPSILON,
             )
-            p_scales[r, h] = p_scale
+            p_scales[r, i] = p_scale
 
-        def scale_bias(r, parts):
-            scaled = turns.tile([P, PAIR, HEADS, D_HEAD], F32, name="bias_scaled", tag=turn_of(r), align_bytes=64)
-            for engine, heads in parts:
-                engine.tensor_scalar(
-                    out=scaled[:, :, heads, :],
-                    in0=bias_rows[r][:, :, heads, :],
-                    scalar1=1.0 / math.sqrt(2.0),
-                    scalar2=0.0,
-                    op0=ALU.mult,
-                    op1=ALU.add,
+        def scale_bias(r, engine, heads):
+            if r not in bias_scaled:
+                bias_scaled[r] = turns.tile(
+                    [P, PAIR, HEADS, D_HEAD], F32, name="bias_scaled", tag=turn_of(r), align_bytes=64
                 )
-            bias_scaled[r] = scaled
+            engine.tensor_scalar(
+                out=bias_scaled[r][:, :, heads, :],
+                in0=bias_rows[r][:, :, heads, :],
+                scalar1=1.0 / math.sqrt(2.0),
+                scalar2=0.0,
+                op0=ALU.mult,
+                op1=ALU.add,
+            )
 
-        def blend(r, h, t):
-            if t == 0:
-                u_rows[r, h] = work.tile([P, PAIR * D_HEAD], BF16, name="u_rows")
+        def blend(r, j):
+            t, h = parts_of(r)[j]
+            i = j // 2
+            if j % 2 == 0:
+                u_rows[r, i] = work.tile([P, 2 * D_HEAD], BF16, name="u_rows")
             nc.vector.scalar_tensor_tensor(
-                out=u_rows[r, h][:, block(t, D_HEAD)],
-                in0=p_banks[r, h, t][:],
-                scalar=p_scales[r, h][:, t : t + 1],
+                out=u_rows[r, i][:, block(j % 2, D_HEAD)],
+                in0=p_banks[r, j][:],
+                scalar=p_scales[r, i][:, j % 2 : j % 2 + 1],
                 in1=bias_scaled[r][:, t, h, :],
                 op0=ALU.mult,
                 op1=ALU.add,
             )
 
-        def transpose_u(r, h):
-            bank = psum_ut.tile([P, PAIR, HALVES, P], F32, name="ut_bank")
-            words = u_rows[r, h][:].bitcast(F32)
-            for t in range(PAIR):
+        def transpose_u(r, first, count, pool, tag):
+            bank = pool.tile([P, count, HALVES, P], F32, name="ut_bank", tag=tag)
+            for j in range(first, first + count):
+                words = u_rows[r, j // 2][:].bitcast(F32)
                 for half in range(HALVES):
-                    nc.tensor.transpose(bank[:, t, half, :], words[:, block(t * HALVES + half, P)], identity[:])
-            ut_banks[r, h] = bank
+                    nc.tensor.transpose(
+                        bank[:, j - first, half, :], words[:, block(j % 2 * HALVES + half, P)], identity[:]
+                    )
+            ut_banks[r, first] = bank
 
-        def fetch_u(r, h, copy):
-            if h == 0:
-                u_grouped[r] = work.tile([P, HEADS * PAIR * P * PACK], BF16, name="u_grouped", align_bytes=64)
+        def fetch_u(r, first, count, copy):
+            if first == 0:
+                u_grouped[r] = work.tile([P, 4 * P * PACK], BF16, name="u_grouped", align_bytes=64)
             copy(
                 out=u_grouped[r][:]
-                .bitcast(F32)[:, block(h, PAIR * P * HALVES)]
-                .rearrange("p (t r half) -> p t r half", t=PAIR, half=HALVES),
-                in_=ut_banks[r, h][:].rearrange("p t half r -> p t r half"),
+                .bitcast(F32)[:, first * P * HALVES : (first + count) * P * HALVES]
+                .rearrange("p (j r half) -> p j r half", j=count, half=HALVES),
+                in_=ut_banks[r, first][:].rearrange("p j half r -> p j r half"),
             )
 
-        def quantise_u(r, part, parts):
-            if part == 0:
-                u_codes[r] = work.tile([P, HEADS * PAIR * P], U32, name="u_codes", align_bytes=64)
-                u_scales[r] = work.tile([P, HEADS * PAIR * P], U8, name="u_scales", align_bytes=64)
-            words = block(part, HEADS * PAIR * P // parts)
+        def quantise_u(r, i, pieces):
+            if i == 0:
+                u_codes[r] = work.tile([P, 4 * P], U32, name="u_codes", align_bytes=64)
+                u_scales[r] = work.tile([P, 4 * P], U8, name="u_scales", align_bytes=64)
+            words = block(i, 4 * P // pieces)
             nc.vector.quantize_mx(
                 out=u_codes[r][:, words].bitcast(FP8X4),
                 scales=u_scales[r][:, words],
-                in_=u_grouped[r][:, block(part, HEADS * PAIR * P * PACK // parts)],
+                in_=u_grouped[r][:, block(i, 4 * P * PACK // pieces)],
             )
 
-        def project_head(r, h, bank):
-            for t in range(PAIR):
+        def project_heads(r, i, bank):
+            for j in (2 * i, 2 * i + 1):
+                t, h = parts_of(r)[j]
                 nc.tensor.matmul_mx(
                     out=bank[:, t, h, :],
-                    lhsT=u_codes[r][:, block(h * PAIR + t, P)].bitcast(FP8X4),
-                    lhsT_scale=u_scales[r][:, block(h * PAIR + t, P)],
+                    lhsT=u_codes[r][:, block(j, P)].bitcast(FP8X4),
+                    lhsT_scale=u_scales[r][:, block(j, P)],
                     rhs=k_codes[:, block(h, F_OUT)].bitcast(FP8X4),
                     rhs_scale=k_scales[:, block(h, F_OUT)],
                     start=True,
                     stop=True,
                 )
+            y_banks[r, i] = bank
 
-        def project_heads(r):
-            bank = psum_y.tile([P, PAIR, HEADS, F_OUT], F32, name="y_bank")
-            for h in range(HEADS):
-                project_head(r, h, bank)
-            y_banks[r] = bank
+        def y_bank(pool, tag):
+            return pool.tile([P, PAIR, HEADS, F_OUT], F32, name="y_bank", tag=tag)
 
-        def fetch_y(r, t, copy):
+        def fetch_y(r, copy):
+            y_rows[r] = work.tile([P, PAIR, HEADS * F_OUT], F32, name="y_rows")
+            copy(out=y_rows[r][:], in_=y_banks[r, 0][:].rearrange("p t h f -> p t (h f)"))
+
+        def store_y_tile(r, t, copy):
             if t == 0:
                 y_rows[r] = work.tile([P, PAIR, HEADS * F_OUT], F32, name="y_rows")
-            copy(out=y_rows[r][:, t, :], in_=y_banks[r][:, t, :, :].rearrange("p h f -> p (h f)"))
+            copy(out=y_rows[r][:, t, :], in_=y_banks[r, t][:, t, :, :].rearrange("p h f -> p (h f)"))
+            nc.sync.dma_start(out=out_view[:, r * PAIR + t, :], in_=y_rows[r][:, t, :])
 
         def store_y(r):
             nc.sync.dma_start(out=out_view[:, tiles_of(r), :], in_=y_rows[r][:])
@@ -223,8 +238,8 @@ def tile_grouplinearblock_pa_t_kernel(tc, x, norm_bias, w_lin, kernel, out):
         def group_w(h):
             w_grouped[h] = consts.tile([P, D_HEAD, PACK], BF16, name="w_grouped%d" % h, align_bytes=64)
             for copy, columns in (
-                (nc.vector.tensor_copy, slice(0, W_SPLIT)),
-                (nc.scalar.copy, slice(W_SPLIT, D_HEAD)),
+                (nc.vector.tensor_copy, slice(0, W_SPLIT[h])),
+                (nc.scalar.copy, slice(W_SPLIT[h], D_HEAD)),
             ):
                 copy(
                     out=w_grouped[h][:, columns, :].rearrange("p (c i) t -> p c t i", i=4),
@@ -252,34 +267,43 @@ def tile_grouplinearblock_pa_t_kernel(tc, x, norm_bias, w_lin, kernel, out):
             if live(r + LOAD_AHEAD):
                 load_x(r + LOAD_AHEAD)
                 load_bias(r + LOAD_AHEAD)
-            sum_squares(r, 0, 0)
-            sum_squares(r, 0, 1)
-            sum_squares(r, 1, 0)
-            scale_of_p(r, 0)
-            sum_squares(r, 1, 1)
+            y_by_vector = (r % 3 == 1 or not live(r + 2)) and live(r + 1)
+            sum_squares(r, 0)
+            sum_squares(r, 1)
+            if r in (0, ROUNDS - 1):
+                scale_of_p(r, 0)
+                sum_squares(r, 2)
+            else:
+                sum_squares(r, 2)
+                scale_of_p(r, 0)
+            sum_squares(r, 3)
             if live(r - 1):
-                fetch_u(r - 1, 0, nc.scalar.copy)
+                fetch_u(r - 1, 0, 2, nc.scalar.copy)
             scale_of_p(r, 1)
             if live(r - 1):
-                fetch_u(r - 1, 1, nc.scalar.copy)
-            if live(r - 2):
-                fetch_y(r - 2, 0, nc.scalar.copy)
-            for h in range(HEADS):
-                for t in range(PAIR):
-                    blend(r, h, t)
-                    if live(r + 1):
-                        project(r + 1, h, t)
-                if h == 0 and live(r + 2):
+                fetch_u(r - 1, 2, 2, nc.scalar.copy)
+            if live(r - 2) and not y_by_vector:
+                fetch_y(r - 2, nc.scalar.copy)
+            for j in range(4):
+                blend(r, j)
+                if live(r + 1):
+                    project(r + 1, j)
+                if j == 1 and live(r + 2):
                     fetch_x(r + 2, nc.vector.tensor_copy)
-                if h == 1 and live(r - 2):
-                    fetch_y(r - 2, 1, nc.vector.tensor_copy)
-                    store_y(r - 2)
+                if j == 3 and live(r - 2) and y_by_vector:
+                    fetch_y(r - 2, nc.vector.tensor_copy)
+            if live(r - 2):
+                store_y(r - 2)
             if live(r + 1):
-                scale_bias(r + 1, [(nc.gpsimd, slice(0, HEADS))])
-            for h in range(HEADS):
-                transpose_u(r, h)
+                scale_bias(r + 1, nc.gpsimd, slice(0, HEADS))
+            transpose_u(r, 0, 2, psum_ut, "ut_bank")
+            if r < ROUNDS - 1:
+                transpose_u(r, 2, 2, psum_ut, "ut_bank")
+            else:
+                for j in (2, 3):
+                    transpose_u(r, j, 1, psum_p, "p_bank")
             if live(r + 3):
-                transpose_x(r + 3)
+                transpose_x(r + 3, psum_xt, "xt_bank")
             if live(r - 1):
                 quantise_u(r - 1, 0, 1)
             else:
@@ -287,7 +311,9 @@ def tile_grouplinearblock_pa_t_kernel(tc, x, norm_bias, w_lin, kernel, out):
             if live(r + 2):
                 quantise_x(r + 2)
             if live(r - 1):
-                project_heads(r - 1)
+                bank = y_bank(psum_y, "y_bank")
+                for i in range(2):
+                    project_heads(r - 1, i, bank)
 
         w_rows = {}
         for h in range(HEADS):
@@ -300,8 +326,8 @@ def tile_grouplinearblock_pa_t_kernel(tc, x, norm_bias, w_lin, kernel, out):
         identity = consts.tile([P, P], F32, name="identity")
         one = consts.tile([P, 1], F32, name="one")
 
-        load_w(0)
         load_x(0)
+        load_w(0)
         load_x(1)
         load_w(1)
         load_bias(0)
@@ -317,32 +343,34 @@ def tile_grouplinearblock_pa_t_kernel(tc, x, norm_bias, w_lin, kernel, out):
         nc.vector.memset(one[:], 1.0)
         nc.scalar.activation(out=one[:], in_=one[:], func=ACT.Abs_reciprocal_sqrt)
 
-        group_w(0)
-        transpose_x(0)
+        transpose_x(0, psum_xt, "xt_bank")
         fetch_x(0, nc.scalar.copy)
-        quantise_w(0)
-        transpose_x(1)
-        fetch_x(1, nc.scalar.copy)
+        group_w(0)
         quantise_x(0)
-        for t in range(PAIR):
-            project(0, 0, t)
+        transpose_x(1, psum_ut, "ut_bank")
+        fetch_x(1, nc.scalar.copy)
+        quantise_w(0)
+        for j in range(2):
+            project(0, j)
         group_w(1)
-        quantise_w(1)
-        for t in range(PAIR):
-            project(0, 1, t)
-        transpose_x(2)
-        scale_bias(0, [(nc.vector, slice(0, 1)), (nc.vector, slice(1, 2))])
         quantise_x(1)
+        quantise_w(1)
+        for j in range(2, 4):
+            project(0, j)
+        transpose_x(2, psum_xt, "xt_bank")
+        for h in range(HEADS):
+            scale_bias(0, nc.vector, slice(h, h + 1))
         for r in range(ROUNDS):
             step(r)
         last = ROUNDS - 1
-        fetch_u(last, 0, nc.scalar.copy)
-        fetch_u(last, 1, nc.vector.tensor_copy)
-        fetch_y(last - 1, 0, nc.scalar.copy)
-        fetch_y(last - 1, 1, nc.vector.tensor_copy)
+        fetch_u(last, 0, 2, nc.scalar.copy)
+        fetch_u(last, 2, 1, nc.scalar.copy)
+        fetch_u(last, 3, 1, nc.vector.tensor_copy)
+        quantise_u(last, 0, 2)
+        fetch_y(last - 1, nc.scalar.copy)
         store_y(last - 1)
-        quantise_u(last, 0, 1)
-        project_heads(last)
-        fetch_y(last, 0, nc.scalar.copy)
-        fetch_y(last, 1, nc.vector.tensor_copy)
-        store_y(last)
+        quantise_u(last, 1, 2)
+        for i in range(2):
+            project_heads(last, i, y_bank(psum_p, "p_bank"))
+        for t, copy in ((0, nc.scalar.copy), (1, nc.vector.tensor_copy)):
+            store_y_tile(last, t, copy)

@@ -288,10 +288,10 @@ def tile_grouplinearblock_pa_t_kernel(tc, x, norm_bias, w_lin, kernel, out):
                 blend(r, j)
                 if live(r + 1):
                     project(r + 1, j)
-                if j == 1 and live(r + 2):
-                    fetch_x(r + 2, nc.vector.tensor_copy)
-                if j == 3 and live(r - 2) and y_by_vector:
-                    fetch_y(r - 2, nc.vector.tensor_copy)
+            if live(r + 2):
+                fetch_x(r + 2, nc.vector.tensor_copy)
+            if live(r - 2) and y_by_vector:
+                fetch_y(r - 2, nc.vector.tensor_copy)
             if live(r - 2):
                 store_y(r - 2)
             if live(r + 1):

@@ -25,6 +25,8 @@ HALVES = 2
 TILES = TOKENS // P
 PAIR = 2
 ROUNDS = TILES // PAIR
+Y_COLUMNS = PAIR * HEADS * F_OUT
+Y_SPLIT = 320
 LOAD_AHEAD = 6
 TURNS = 3
 W_SPLIT = (384, 336)
@@ -50,6 +52,7 @@ def tile_grouplinearblock_pa_t_kernel(tc, x, norm_bias, w_lin, kernel, out):
         out_view = out.rearrange("(p t) f -> p t f", t=TILES)
 
         x_rows, bias_rows, xt_banks, x_grouped, x_codes, x_scales, w_grouped = {}, {}, {}, {}, {}, {}, {}
+        k_grouped = {}
         bias_scaled, p_banks, sums_sq, p_scales, u_rows, ut_banks = {}, {}, {}, {}, {}, {}
         u_grouped, u_codes, u_scales, y_banks, y_rows = {}, {}, {}, {}, {}
 
@@ -209,18 +212,20 @@ def tile_grouplinearblock_pa_t_kernel(tc, x, norm_bias, w_lin, kernel, out):
         def y_bank(pool, tag):
             return pool.tile([P, PAIR, HEADS, F_OUT], F32, name="y_bank", tag=tag)
 
-        def fetch_y(r, copy):
-            y_rows[r] = work.tile([P, PAIR, HEADS * F_OUT], F32, name="y_rows")
-            copy(out=y_rows[r][:], in_=y_banks[r, 0][:].rearrange("p t h f -> p t (h f)"))
+        def fetch_y(r, copy, columns):
+            if r not in y_rows:
+                y_rows[r] = work.tile([P, Y_COLUMNS], F32, name="y_rows")
+            copy(out=y_rows[r][:, columns], in_=y_banks[r, 0][:].rearrange("p t h f -> p (t h f)")[:, columns])
 
         def store_y_tile(r, t, copy):
             if t == 0:
-                y_rows[r] = work.tile([P, PAIR, HEADS * F_OUT], F32, name="y_rows")
-            copy(out=y_rows[r][:, t, :], in_=y_banks[r, t][:, t, :, :].rearrange("p h f -> p (h f)"))
-            nc.sync.dma_start(out=out_view[:, r * PAIR + t, :], in_=y_rows[r][:, t, :])
+                y_rows[r] = work.tile([P, Y_COLUMNS], F32, name="y_rows")
+            columns = block(t, HEADS * F_OUT)
+            copy(out=y_rows[r][:, columns], in_=y_banks[r, t][:, t, :, :].rearrange("p h f -> p (h f)"))
+            nc.sync.dma_start(out=out_view[:, r * PAIR + t, :], in_=y_rows[r][:, columns])
 
         def store_y(r):
-            nc.sync.dma_start(out=out_view[:, tiles_of(r), :], in_=y_rows[r][:])
+            nc.sync.dma_start(out=out_view[:, tiles_of(r), :], in_=y_rows[r][:].rearrange("p (t c) -> p t c", t=PAIR))
 
         def load_w(h):
             w_view = w_lin.rearrange("(half q e) c -> half q e c", half=HALVES, e=2)
@@ -253,12 +258,20 @@ def tile_grouplinearblock_pa_t_kernel(tc, x, norm_bias, w_lin, kernel, out):
                 in_=w_grouped[h][:].rearrange("p c t -> p (c t)"),
             )
 
-        def quantise_kernel():
-            grouped = consts.tile([P, HEADS, F_OUT, PACK], BF16, name="k_grouped", align_bytes=64)
-            nc.vector.tensor_copy(out=grouped[:], in_=k_rows[:].rearrange("p h t f -> p h f t"))
-            nc.vector.quantize_mx(
-                out=k_codes[:].bitcast(FP8X4), scales=k_scales[:], in_=grouped[:].rearrange("p h f t -> p (h f t)")
+        def group_kernel(h):
+            k_grouped[h] = consts.tile([P, F_OUT, PACK], BF16, name="k_grouped%d" % h, align_bytes=64)
+            nc.scalar.copy(
+                out=k_grouped[h][:].rearrange("p (f i) t -> p f t i", i=4),
+                in_=k_rows[:, h, :, :].rearrange("p t (f i) -> p f t i", i=4),
             )
+
+        def quantise_kernel():
+            for h in range(HEADS):
+                nc.vector.quantize_mx(
+                    out=k_codes[:, block(h, F_OUT)].bitcast(FP8X4),
+                    scales=k_scales[:, block(h, F_OUT)],
+                    in_=k_grouped[h][:].rearrange("p f t -> p (f t)"),
+                )
 
         def step(r):
             def live(i):
@@ -267,7 +280,6 @@ def tile_grouplinearblock_pa_t_kernel(tc, x, norm_bias, w_lin, kernel, out):
             if live(r + LOAD_AHEAD):
                 load_x(r + LOAD_AHEAD)
                 load_bias(r + LOAD_AHEAD)
-            y_by_vector = (r % 3 == 1 or not live(r + 2)) and live(r + 1)
             sum_squares(r, 0)
             sum_squares(r, 1)
             if r in (0, ROUNDS - 1):
@@ -282,16 +294,19 @@ def tile_grouplinearblock_pa_t_kernel(tc, x, norm_bias, w_lin, kernel, out):
             scale_of_p(r, 1)
             if live(r - 1):
                 fetch_u(r - 1, 2, 2, nc.scalar.copy)
-            if live(r - 2) and not y_by_vector:
-                fetch_y(r - 2, nc.scalar.copy)
+            y_split = Y_SPLIT if live(r + 1) else Y_COLUMNS
+            if live(r - 2):
+                fetch_y(r - 2, nc.scalar.copy, slice(0, y_split))
+            if r < HEADS:
+                group_kernel(r)
             for j in range(4):
                 blend(r, j)
                 if live(r + 1):
                     project(r + 1, j)
             if live(r + 2):
                 fetch_x(r + 2, nc.vector.tensor_copy)
-            if live(r - 2) and y_by_vector:
-                fetch_y(r - 2, nc.vector.tensor_copy)
+            if live(r - 2) and y_split < Y_COLUMNS:
+                fetch_y(r - 2, nc.vector.tensor_copy, slice(y_split, Y_COLUMNS))
             if live(r - 2):
                 store_y(r - 2)
             if live(r + 1):
@@ -306,7 +321,7 @@ def tile_grouplinearblock_pa_t_kernel(tc, x, norm_bias, w_lin, kernel, out):
                 transpose_x(r + 3, psum_xt, "xt_bank")
             if live(r - 1):
                 quantise_u(r - 1, 0, 1)
-            else:
+            if r == 1:
                 quantise_kernel()
             if live(r + 2):
                 quantise_x(r + 2)
@@ -333,8 +348,8 @@ def tile_grouplinearblock_pa_t_kernel(tc, x, norm_bias, w_lin, kernel, out):
         load_bias(0)
         load_x(2)
         load_bias(1)
-        load_x(3)
         load_kernel()
+        load_x(3)
         for r in range(2, LOAD_AHEAD):
             load_bias(r)
             if r + 2 < LOAD_AHEAD:
@@ -364,10 +379,10 @@ def tile_grouplinearblock_pa_t_kernel(tc, x, norm_bias, w_lin, kernel, out):
             step(r)
         last = ROUNDS - 1
         fetch_u(last, 0, 2, nc.scalar.copy)
-        fetch_u(last, 2, 1, nc.scalar.copy)
-        fetch_u(last, 3, 1, nc.vector.tensor_copy)
+        for j in (2, 3):
+            fetch_u(last, j, 1, nc.scalar.copy)
         quantise_u(last, 0, 2)
-        fetch_y(last - 1, nc.scalar.copy)
+        fetch_y(last - 1, nc.scalar.copy, slice(0, Y_COLUMNS))
         store_y(last - 1)
         quantise_u(last, 1, 2)
         for i in range(2):

@@ -227,6 +227,10 @@ def tile_grouplinearblock_pa_t_kernel(tc, x, norm_bias, w_lin, kernel, out):
         def store_y(r):
             nc.sync.dma_start(out=out_view[:, tiles_of(r), :], in_=y_rows[r][:].rearrange("p (t c) -> p t c", t=PAIR))
 
+        def keep_warm(bank, count):
+            for i in range(count):
+                nc.tensor.matmul(out=bank, lhsT=zeros[:, block(0, P)], rhs=zeros[:], start=True, stop=True)
+
         def load_w(h):
             w_view = w_lin.rearrange("(half q e) c -> half q e c", half=HALVES, e=2)
             for half in range(HALVES):
@@ -282,7 +286,7 @@ def tile_grouplinearblock_pa_t_kernel(tc, x, norm_bias, w_lin, kernel, out):
                 load_bias(r + LOAD_AHEAD)
             sum_squares(r, 0)
             sum_squares(r, 1)
-            if r in (0, ROUNDS - 1):
+            if r == 0:
                 scale_of_p(r, 0)
                 sum_squares(r, 2)
             else:
@@ -294,29 +298,21 @@ def tile_grouplinearblock_pa_t_kernel(tc, x, norm_bias, w_lin, kernel, out):
             scale_of_p(r, 1)
             if live(r - 1):
                 fetch_u(r - 1, 2, 2, nc.scalar.copy)
-            y_split = Y_SPLIT if live(r + 1) else Y_COLUMNS
             if live(r - 2):
-                fetch_y(r - 2, nc.scalar.copy, slice(0, y_split))
+                fetch_y(r - 2, nc.scalar.copy, slice(0, Y_SPLIT))
             if r < HEADS:
                 group_kernel(r)
             for j in range(4):
                 blend(r, j)
-                if live(r + 1):
-                    project(r + 1, j)
+                project(r + 1, j)
             if live(r + 2):
                 fetch_x(r + 2, nc.vector.tensor_copy)
-            if live(r - 2) and y_split < Y_COLUMNS:
-                fetch_y(r - 2, nc.vector.tensor_copy, slice(y_split, Y_COLUMNS))
             if live(r - 2):
+                fetch_y(r - 2, nc.vector.tensor_copy, slice(Y_SPLIT, Y_COLUMNS))
                 store_y(r - 2)
-            if live(r + 1):
-                scale_bias(r + 1, nc.gpsimd, slice(0, HEADS))
-            transpose_u(r, 0, 2, psum_ut, "ut_bank")
-            if r < ROUNDS - 1:
-                transpose_u(r, 2, 2, psum_ut, "ut_bank")
-            else:
-                for j in (2, 3):
-                    transpose_u(r, j, 1, psum_p, "p_bank")
+            scale_bias(r + 1, nc.gpsimd, slice(0, HEADS))
+            for first in (0, 2):
+                transpose_u(r, first, 2, psum_ut, "ut_bank")
             if live(r + 3):
                 transpose_x(r + 3, psum_xt, "xt_bank")
             if live(r - 1):
@@ -340,6 +336,7 @@ def tile_grouplinearblock_pa_t_kernel(tc, x, norm_bias, w_lin, kernel, out):
         k_scales = consts.tile([P, HEADS * F_OUT], U8, name="k_scales", align_bytes=64)
         identity = consts.tile([P, P], F32, name="identity")
         one = consts.tile([P, 1], F32, name="one")
+        zeros = consts.tile([P, D_HEAD], BF16, name="zeros")
 
         load_x(0)
         load_w(0)
@@ -355,14 +352,19 @@ def tile_grouplinearblock_pa_t_kernel(tc, x, norm_bias, w_lin, kernel, out):
             if r + 2 < LOAD_AHEAD:
                 load_x(r + 2)
         make_identity(nc, identity[:])
+        nc.vector.memset(zeros[:], 0.0)
         nc.vector.memset(one[:], 1.0)
         nc.scalar.activation(out=one[:], in_=one[:], func=ACT.Abs_reciprocal_sqrt)
 
+        warm = psum_p.tile([P, D_HEAD], F32, name="warm", tag="p_bank")
+        keep_warm(warm[:], 4)
         transpose_x(0, psum_xt, "xt_bank")
+        keep_warm(warm[:], 2)
         fetch_x(0, nc.scalar.copy)
         group_w(0)
         quantise_x(0)
         transpose_x(1, psum_ut, "ut_bank")
+        keep_warm(warm[:], 2)
         fetch_x(1, nc.scalar.copy)
         quantise_w(0)
         for j in range(2):
@@ -375,17 +377,39 @@ def tile_grouplinearblock_pa_t_kernel(tc, x, norm_bias, w_lin, kernel, out):
         transpose_x(2, psum_xt, "xt_bank")
         for h in range(HEADS):
             scale_bias(0, nc.vector, slice(h, h + 1))
-        for r in range(ROUNDS):
+        for r in range(ROUNDS - 1):
             step(r)
         last = ROUNDS - 1
+        for j in range(2):
+            sum_squares(last, j)
+        scale_of_p(last, 0)
+        for j in range(2, 4):
+            sum_squares(last, j)
+        scale_of_p(last, 1)
+        for first in (0, 2):
+            fetch_u(last - 1, first, 2, nc.scalar.copy)
+        for j in range(4):
+            blend(last, j)
+        bank = y_bank(psum_xt, "xt_bank")
+        flat = bank[:].rearrange("p t h f -> p (t h f)")
+        keep_warm(flat, 1)
+        transpose_u(last, 0, 2, psum_p, "p_bank")
+        transpose_u(last, 2, 1, psum_p, "p_bank")
+        keep_warm(flat, 1)
+        transpose_u(last, 3, 1, psum_p, "p_bank")
+        quantise_u(last - 1, 0, 1)
+        for i in range(2):
+            project_heads(last - 1, i, bank)
         fetch_u(last, 0, 2, nc.scalar.copy)
         for j in (2, 3):
             fetch_u(last, j, 1, nc.scalar.copy)
         quantise_u(last, 0, 2)
+        project_heads(last, 0, y_bank(psum_p, "p_bank"))
+        fetch_y(last - 2, nc.vector.tensor_copy, slice(0, Y_COLUMNS))
+        store_y(last - 2)
+        quantise_u(last, 1, 2)
+        project_heads(last, 1, y_bank(psum_p, "p_bank"))
         fetch_y(last - 1, nc.scalar.copy, slice(0, Y_COLUMNS))
         store_y(last - 1)
-        quantise_u(last, 1, 2)
-        for i in range(2):
-            project_heads(last, i, y_bank(psum_p, "p_bank"))
-        for t, copy in ((0, nc.scalar.copy), (1, nc.vector.tensor_copy)):
+        for t, copy in ((0, nc.vector.tensor_copy), (1, nc.scalar.copy)):
             store_y_tile(last, t, copy)

import math
from contextlib import ExitStack

import concourse.mybir as mybir
from concourse.masks import make_identity

F32 = mybir.dt.float32
BF16 = mybir.dt.bfloat16
U32 = mybir.dt.uint32
U8 = mybir.dt.uint8
FP8X4 = mybir.dt.float8_e4m3fn_x4
ACT = mybir.ActivationFunctionType
ALU = mybir.AluOpType

P = 128
PACK = 4
TOKENS = 4096
K_IN = 512
HEADS = 2
D_HEAD = 512
F_OUT = 128
EPSILON = 1e-06

HALVES = 2
TILES = TOKENS // P
PAIR = 2
ROUNDS = TILES // PAIR
Y_COLUMNS = PAIR * HEADS * F_OUT
Y_SPLIT = 320
LOAD_AHEAD = 6
TURNS = 3
W_SPLIT = (384, 336)

FLOPS = 2 * TOKENS * K_IN * HEADS * D_HEAD + 2 * TOKENS * HEADS * D_HEAD * F_OUT


def tile_grouplinearblock_pa_t_kernel(tc, x, norm_bias, w_lin, kernel, out):
    nc = tc.nc
    with ExitStack() as ctx:
        ctx.enter_context(tc.manual_schedule())
        consts = ctx.enter_context(tc.tile_pool(name="consts", bufs=1))
        loads = ctx.enter_context(tc.tile_pool(name="loads", bufs=LOAD_AHEAD + 2))
        work = ctx.enter_context(tc.tile_pool(name="work", bufs=4))
        turns = ctx.enter_context(tc.tile_pool(name="turns", bufs=1))
        psum_p = ctx.enter_context(tc.psum_pool(name="psum_p", bufs=HEADS * PAIR))
        psum_ut = ctx.enter_context(tc.psum_pool(name="psum_ut", bufs=HEADS))
        psum_xt = ctx.enter_context(tc.psum_pool(name="psum_xt", bufs=1))
        psum_y = ctx.enter_context(tc.psum_pool(name="psum_y", bufs=1))

        x_view = x.rearrange("(p t) k -> p t k", t=TILES)
        bias_view = norm_bias.rearrange("(p t) h d -> p t (h d)", t=TILES)
        out_view = out.rearrange("(p t) f -> p t f", t=TILES)

        x_rows, bias_rows, xt_banks, x_grouped, x_codes, x_scales, w_grouped = {}, {}, {}, {}, {}, {}, {}
        k_grouped = {}
        bias_scaled, p_banks, sums_sq, p_scales, u_rows, ut_banks = {}, {}, {}, {}, {}, {}
        u_grouped, u_codes, u_scales, y_banks, y_rows = {}, {}, {}, {}, {}

        def parts_of(r):
            if r == 0:
                return [(t, h) for h in range(HEADS) for t in range(PAIR)]
            return [(t, h) for t in range(PAIR) for h in range(HEADS)]

        def turn_of(r):
            return "turn%d" % (r % TURNS)

        def tiles_of(r):
            return slice(r * PAIR, (r + 1) * PAIR)

        def block(i, width):
            return slice(i * width, (i + 1) * width)

        def load_x(r):
            rows = loads.tile([P, PAIR * K_IN], BF16, name="x_rows")
            nc.sync.dma_start(out=rows[:].rearrange("p (t k) -> p t k", t=PAIR), in_=x_view[:, tiles_of(r), :])
            x_rows[r] = rows

        def load_bias(r):
            rows = loads.tile([P, PAIR, HEADS, D_HEAD], BF16, name="bias_rows")
            nc.sync.dma_start(out=rows[:].rearrange("p t h d -> p t (h d)"), in_=bias_view[:, tiles_of(r), :])
            bias_rows[r] = rows

        def transpose_x(r, pool, tag):
            bank = pool.tile([P, PAIR, HALVES, P], F32, name="xt_bank", tag=tag)
            words = x_rows[r][:].bitcast(F32)
            for t in range(PAIR):
                for half in range(HALVES):
                    nc.tensor.transpose(bank[:, t, half, :], words[:, block(t * HALVES + half, P)], identity[:])
            xt_banks[r] = bank

        def fetch_x(r, copy):
            grouped = turns.tile([P, PAIR * P * PACK], BF16, name="x_grouped", tag=turn_of(r), align_bytes=64)
            copy(
                out=grouped[:].bitcast(F32).rearrange("p (t r half) -> p t r half", t=PAIR, half=HALVES),
                in_=xt_banks[r][:].rearrange("p t half r -> p t r half"),
            )
            x_grouped[r] = grouped

        def quantise_x(r):
            codes = work.tile([P, PAIR * P], U32, name="x_codes", align_bytes=64)
            scales = work.tile([P, PAIR * P], U8, name="x_scales", align_bytes=64)
            nc.vector.quantize_mx(out=codes[:].bitcast(FP8X4), scales=scales[:], in_=x_grouped[r][:])
            x_codes[r], x_scales[r] = codes, scales

        def project(r, j):
            t, h = parts_of(r)[j]
            bank = psum_p.tile([P, D_HEAD], F32, name="p_bank", tag="p_bank")
            nc.tensor.matmul_mx(
                out=bank[:],
                lhsT=x_codes[r][:, block(t, P)].bitcast(FP8X4),
                lhsT_scale=x_scales[r][:, block(t, P)],
                rhs=w_codes[:, block(h, D_HEAD)].bitcast(FP8X4),
                rhs_scale=w_scales[:, block(h, D_HEAD)],
                start=True,
                stop=True,
            )
            p_banks[r, j] = bank

        def sum_squares(r, j):
            i = j // 2
            if j % 2 == 0:
                sums_sq[r, i] = work.tile([P, 2], F32, name="sum_sq")
            squares = work.tile([P, D_HEAD], BF16, name="squares")
            nc.scalar.activation(
                out=squares[:], in_=p_banks[r, j][:], func=ACT.Square, accum_out=sums_sq[r, i][:, j % 2 : j % 2 + 1]
            )

        def scale_of_p(r, i):
            p_scale = work.tile([P, 2], F32, name="p_scale")
            nc.scalar.activation(
                out=p_scale[:],
                in_=sums_sq[r, i][:],
                func=ACT.Abs_reciprocal_sqrt,
                scale=2.0 / D_HEAD,
                bias=2.0 * EPSILON,
            )
            p_scales[r, i] = p_scale

        def scale_bias(r, engine, heads):
            if r not in bias_scaled:
                bias_scaled[r] = turns.tile(
                    [P, PAIR, HEADS, D_HEAD], F32, name="bias_scaled", tag=turn_of(r), align_bytes=64
                )
            engine.tensor_scalar(
                out=bias_scaled[r][:, :, heads, :],
                in0=bias_rows[r][:, :, heads, :],
                scalar1=1.0 / math.sqrt(2.0),
                scalar2=0.0,
                op0=ALU.mult,
                op1=ALU.add,
            )

        def blend(r, j):
            t, h = parts_of(r)[j]
            i = j // 2
            if j % 2 == 0:
                u_rows[r, i] = work.tile([P, 2 * D_HEAD], BF16, name="u_rows")
            nc.vector.scalar_tensor_tensor(
                out=u_rows[r, i][:, block(j % 2, D_HEAD)],
                in0=p_banks[r, j][:],
                scalar=p_scales[r, i][:, j % 2 : j % 2 + 1],
                in1=bias_scaled[r][:, t, h, :],
                op0=ALU.mult,
                op1=ALU.add,
            )

        def transpose_u(r, first, count, pool, tag):
            bank = pool.tile([P, count, HALVES, P], F32, name="ut_bank", tag=tag)
            for j in range(first, first + count):
                words = u_rows[r, j // 2][:].bitcast(F32)
                for half in range(HALVES):
                    nc.tensor.transpose(
                        bank[:, j - first, half, :], words[:, block(j % 2 * HALVES + half, P)], identity[:]
                    )
            ut_banks[r, first] = bank

        def fetch_u(r, first, count, copy):
            if first == 0:
                u_grouped[r] = work.tile([P, 4 * P * PACK], BF16, name="u_grouped", align_bytes=64)
            copy(
                out=u_grouped[r][:]
                .bitcast(F32)[:, first * P * HALVES : (first + count) * P * HALVES]
                .rearrange("p (j r half) -> p j r half", j=count, half=HALVES),
                in_=ut_banks[r, first][:].rearrange("p j half r -> p j r half"),
            )

        def quantise_u(r, i, pieces):
            if i == 0:
                u_codes[r] = work.tile([P, 4 * P], U32, name="u_codes", align_bytes=64)
                u_scales[r] = work.tile([P, 4 * P], U8, name="u_scales", align_bytes=64)
            words = block(i, 4 * P // pieces)
            nc.vector.quantize_mx(
                out=u_codes[r][:, words].bitcast(FP8X4),
                scales=u_scales[r][:, words],
                in_=u_grouped[r][:, block(i, 4 * P * PACK // pieces)],
            )

        def project_heads(r, i, bank):
            for j in (2 * i, 2 * i + 1):
                t, h = parts_of(r)[j]
                nc.tensor.matmul_mx(
                    out=bank[:, t, h, :],
                    lhsT=u_codes[r][:, block(j, P)].bitcast(FP8X4),
                    lhsT_scale=u_scales[r][:, block(j, P)],
                    rhs=k_codes[:, block(h, F_OUT)].bitcast(FP8X4),
                    rhs_scale=k_scales[:, block(h, F_OUT)],
                    start=True,
                    stop=True,
                )
            y_banks[r, i] = bank

        def y_bank(pool, tag):
            return pool.tile([P, PAIR, HEADS, F_OUT], F32, name="y_bank", tag=tag)

        def fetch_y(r, copy, columns):
            if r not in y_rows:
                y_rows[r] = work.tile([P, Y_COLUMNS], F32, name="y_rows")
            copy(out=y_rows[r][:, columns], in_=y_banks[r, 0][:].rearrange("p t h f -> p (t h f)")[:, columns])

        def store_y_tile(r, t, copy):
            if t == 0:
                y_rows[r] = work.tile([P, Y_COLUMNS], F32, name="y_rows")
            columns = block(t, HEADS * F_OUT)
            copy(out=y_rows[r][:, columns], in_=y_banks[r, t][:, t, :, :].rearrange("p h f -> p (h f)"))
            nc.sync.dma_start(out=out_view[:, r * PAIR + t, :], in_=y_rows[r][:, columns])

        def store_y(r):
            nc.sync.dma_start(out=out_view[:, tiles_of(r), :], in_=y_rows[r][:].rearrange("p (t c) -> p t c", t=PAIR))

        def keep_warm(bank, count):
            for i in range(count):
                nc.tensor.matmul(out=bank, lhsT=zeros[:, block(0, P)], rhs=zeros[:], start=True, stop=True)

        def load_w(h):
            w_view = w_lin.rearrange("(half q e) c -> half q e c", half=HALVES, e=2)
            for half in range(HALVES):
                nc.sync.dma_start(
                    out=w_rows[h][:, block(half, 2), :], in_=w_view[half][:, :, block(h, D_HEAD)]
                )

        def load_kernel():
            k_view = kernel.rearrange("h (half q e) f -> h half q e f", half=HALVES, e=2)
            for h in range(HEADS):
                for half in range(HALVES):
                    nc.sync.dma_start(out=k_rows[:, h, block(half, 2), :], in_=k_view[h, half])

        def group_w(h):
            w_grouped[h] = consts.tile([P, D_HEAD, PACK], BF16, name="w_grouped%d" % h, align_bytes=64)
            for copy, columns in (
                (nc.vector.tensor_copy, slice(0, W_SPLIT[h])),
                (nc.scalar.copy, slice(W_SPLIT[h], D_HEAD)),
            ):
                copy(
                    out=w_grouped[h][:, columns, :].rearrange("p (c i) t -> p c t i", i=4),
                    in_=w_rows[h][:, :, columns].rearrange("p t (c i) -> p c t i", i=4),
                )

        def quantise_w(h):
            nc.vector.quantize_mx(
                out=w_codes[:, block(h, D_HEAD)].bitcast(FP8X4),
                scales=w_scales[:, block(h, D_HEAD)],
                in_=w_grouped[h][:].rearrange("p c t -> p (c t)"),
            )

        def group_kernel(h):
            k_grouped[h] = consts.tile([P, F_OUT, PACK], BF16, name="k_grouped%d" % h, align_bytes=64)
            nc.scalar.copy(
                out=k_grouped[h][:].rearrange("p (f i) t -> p f t i", i=4),
                in_=k_rows[:, h, :, :].rearrange("p t (f i) -> p f t i", i=4),
            )

        def quantise_kernel():
            for h in range(HEADS):
                nc.vector.quantize_mx(
                    out=k_codes[:, block(h, F_OUT)].bitcast(FP8X4),
                    scales=k_scales[:, block(h, F_OUT)],
                    in_=k_grouped[h][:].rearrange("p f t -> p (f t)"),
                )

        def step(r):
            def live(i):
                return 0 <= i < ROUNDS

            if live(r + LOAD_AHEAD):
                load_x(r + LOAD_AHEAD)
                load_bias(r + LOAD_AHEAD)
            sum_squares(r, 0)
            sum_squares(r, 1)
            if r == 0:
                scale_of_p(r, 0)
                sum_squares(r, 2)
            else:
                sum_squares(r, 2)
                scale_of_p(r, 0)
            sum_squares(r, 3)
            if live(r - 1):
                fetch_u(r - 1, 0, 2, nc.scalar.copy)
            scale_of_p(r, 1)
            if live(r - 1):
                fetch_u(r - 1, 2, 2, nc.scalar.copy)
            if live(r - 2):
                fetch_y(r - 2, nc.scalar.copy, slice(0, Y_SPLIT))
            if r < HEADS:
                group_kernel(r)
            for j in range(4):
                blend(r, j)
                project(r + 1, j)
            if live(r + 2):
                fetch_x(r + 2, nc.vector.tensor_copy)
            if live(r - 2):
                fetch_y(r - 2, nc.vector.tensor_copy, slice(Y_SPLIT, Y_COLUMNS))
                store_y(r - 2)
            scale_bias(r + 1, nc.gpsimd, slice(0, HEADS))
            for first in (0, 2):
                transpose_u(r, first, 2, psum_ut, "ut_bank")
            if live(r + 3):
                transpose_x(r + 3, psum_xt, "xt_bank")
            if live(r - 1):
                quantise_u(r - 1, 0, 1)
            if r == 1:
                quantise_kernel()
            if live(r + 2):
                quantise_x(r + 2)
            if live(r - 1):
                bank = y_bank(psum_y, "y_bank")
                for i in range(2):
                    project_heads(r - 1, i, bank)

        w_rows = {}
        for h in range(HEADS):
            w_rows[h] = consts.tile([P, PACK, D_HEAD], BF16, name="w_rows%d" % h)
        k_rows = consts.tile([P, HEADS, PACK, F_OUT], BF16, name="k_rows")
        w_codes = consts.tile([P, HEADS * D_HEAD], U32, name="w_codes", align_bytes=64)
        w_scales = consts.tile([P, HEADS * D_HEAD], U8, name="w_scales", align_bytes=64)
        k_codes = consts.tile([P, HEADS * F_OUT], U32, name="k_codes", align_bytes=64)
        k_scales = consts.tile([P, HEADS * F_OUT], U8, name="k_scales", align_bytes=64)
        identity = consts.tile([P, P], F32, name="identity")
        one = consts.tile([P, 1], F32, name="one")
        zeros = consts.tile([P, D_HEAD], BF16, name="zeros")

        load_x(0)
        load_w(0)
        load_x(1)
        load_w(1)
        load_bias(0)
        load_x(2)
        load_bias(1)
        load_kernel()
        load_x(3)
        for r in range(2, LOAD_AHEAD):
            load_bias(r)
            if r + 2 < LOAD_AHEAD:
                load_x(r + 2)
        make_identity(nc, identity[:])
        nc.vector.memset(zeros[:], 0.0)
        nc.vector.memset(one[:], 1.0)
        nc.scalar.activation(out=one[:], in_=one[:], func=ACT.Abs_reciprocal_sqrt)

        warm = psum_p.tile([P, D_HEAD], F32, name="warm", tag="p_bank")
        keep_warm(warm[:], 4)
        transpose_x(0, psum_xt, "xt_bank")
        keep_warm(warm[:], 2)
        fetch_x(0, nc.scalar.copy)
        group_w(0)
        quantise_x(0)
        transpose_x(1, psum_ut, "ut_bank")
        keep_warm(warm[:], 2)
        fetch_x(1, nc.scalar.copy)
        quantise_w(0)
        for j in range(2):
            project(0, j)
        group_w(1)
        quantise_x(1)
        quantise_w(1)
        for j in range(2, 4):
            project(0, j)
        transpose_x(2, psum_xt, "xt_bank")
        for h in range(HEADS):
            scale_bias(0, nc.vector, slice(h, h + 1))
        for r in range(ROUNDS - 1):
            step(r)
        last = ROUNDS - 1
        for j in range(2):
            sum_squares(last, j)
        scale_of_p(last, 0)
        for j in range(2, 4):
            sum_squares(last, j)
        scale_of_p(last, 1)
        for first in (0, 2):
            fetch_u(last - 1, first, 2, nc.scalar.copy)
        for j in range(4):
            blend(last, j)
        bank = y_bank(psum_xt, "xt_bank")
        flat = bank[:].rearrange("p t h f -> p (t h f)")
        keep_warm(flat, 1)
        transpose_u(last, 0, 2, psum_p, "p_bank")
        transpose_u(last, 2, 1, psum_p, "p_bank")
        keep_warm(flat, 1)
        transpose_u(last, 3, 1, psum_p, "p_bank")
        quantise_u(last - 1, 0, 1)
        for i in range(2):
            project_heads(last - 1, i, bank)
        fetch_u(last, 0, 2, nc.scalar.copy)
        for j in (2, 3):
            fetch_u(last, j, 1, nc.scalar.copy)
        quantise_u(last, 0, 2)
        project_heads(last, 0, y_bank(psum_p, "p_bank"))
        fetch_y(last - 2, nc.vector.tensor_copy, slice(0, Y_COLUMNS))
        store_y(last - 2)
        quantise_u(last, 1, 2)
        project_heads(last, 1, y_bank(psum_p, "p_bank"))
        fetch_y(last - 1, nc.scalar.copy, slice(0, Y_COLUMNS))
        store_y(last - 1)
        for t, copy in ((0, nc.vector.tensor_copy), (1, nc.scalar.copy)):
            store_y_tile(last, t, copy)
